import numpy as np
import ml_dtypes


def mxq(x, axis, fmt="e4m3"):
    dtype, down = {"e4m3": (ml_dtypes.float8_e4m3fn, 7), "e5m2": (ml_dtypes.float8_e5m2, 14)}[fmt]
    v = np.moveaxis(np.asarray(x, np.float32).astype(ml_dtypes.bfloat16).astype(np.float64), axis, -1)
    blocks = v.reshape(v.shape[:-1] + (-1, 32))
    amax = np.abs(blocks).max(-1, keepdims=True)
    byte = np.maximum(np.where(amax > 0, np.frexp(amax)[1] - 1 + 127, 0) - down, 1)
    scale = np.exp2(byte - 127.0)
    codes = (blocks / scale).astype(np.float32).astype(dtype).astype(np.float64)
    return np.moveaxis((codes * scale).reshape(v.shape), -1, axis)


WIDE = False


def mx_kscale(k):
    if not WIDE:
        return np.ones(k)
    levels = np.array([10, -10, 5, -5, 0])
    a = np.random.permutation(np.resize(levels, k // 512 * 4)).reshape(k // 512, 4)
    idx = np.arange(k)
    return np.exp2(a[idx // 512, idx % 128 // 32])


BF16 = ml_dtypes.bfloat16


def bf(x):
    return np.asarray(x, np.float32).astype(BF16)


def f64(x):
    return np.asarray(x).astype(np.float64)


E2M1 = np.array([0.0, 0.5, 1.0, 1.5, 2.0, 3.0, 4.0, 6.0, -0.0, -0.5, -1.0, -1.5, -2.0, -3.0, -4.0, -6.0])


def pack_weight(w, fmt):
    k, n = w.shape
    w = f64(bf(w)).reshape(k // 32, 32, n)
    amax = np.abs(w).max(1)
    if fmt == "e4m3":
        byte = np.frexp(amax)[1] - 1 + 127 - 7
    else:
        mant, ex = np.frexp(amax / 6.0)
        byte = np.where(mant > 0.5, ex, ex - 1) + 127
    byte = np.clip(np.where(amax > 0, byte, 1), 1, 254)
    scaled = (w * np.exp2(127.0 - byte)[:, None, :]).reshape(k, n).astype(np.float32)
    by_word = np.ascontiguousarray(scaled.reshape(k // 512, 128, 4, n).transpose(0, 1, 3, 2))
    if fmt == "e4m3":
        words = by_word.astype(ml_dtypes.float8_e4m3fn).view(np.uint8)
    else:
        c = by_word.astype(ml_dtypes.float4_e2m1fn).view(np.uint8) & 0xF
        words = c[..., 0::2] | (c[..., 1::2] << 4)
    return np.ascontiguousarray(words), np.ascontiguousarray(byte.astype(np.uint8).reshape(k // 512, 16, n))


def unpack_weight(words, scales, fmt):
    g, p, n, _ = words.shape
    if fmt == "e4m3":
        vals = np.ascontiguousarray(words).view(ml_dtypes.float8_e4m3fn).astype(np.float64)
    else:
        nib = np.empty((g, p, n, 4), np.uint8)
        nib[..., 0::2] = words & 0xF
        nib[..., 1::2] = words >> 4
        vals = E2M1[nib]
    vals = vals * np.repeat(np.exp2(scales.astype(np.float64) - 127.0), 8, axis=1)[..., None]
    return vals.transpose(0, 1, 3, 2).reshape(g * 512, n)


E, B, S, A, H = 7, 1024, 127, 8, 512
P = S + 1


def swish(v):
    return v / (1.0 + np.exp(-v))


def softplus(v):
    return np.log(1.0 + np.exp(v))


def setup_inputs():
    s = mx_kscale(H)
    h3 = bf(swish(np.random.standard_normal((E, B, H))) * s)
    state = bf(np.random.standard_normal((B, S)))
    noise = bf(np.random.standard_normal((E, B, P)))
    W4 = np.random.standard_normal((E, H, H)) * 1.6 / np.sqrt(H) / s[:, None]
    W4_words, W4_scales = pack_weight(W4.reshape(-1, H), "e4m3")
    b4 = bf(np.random.standard_normal((E, H)) * 0.3)
    W5 = np.random.standard_normal((E, H, 2 * P)) * 1.6 / np.sqrt(H)
    W5_words, W5_scales = pack_weight(W5.reshape(-1, 2 * P), "e4m3")
    b5 = bf(np.random.standard_normal((E, 2 * P)) * 0.3)
    max_logvar = bf(0.5 + 0.1 * np.random.standard_normal((1, P)))
    min_logvar = bf(-1.5 + 0.1 * np.random.standard_normal((1, P)))
    return {"h3": h3,
            "state": state,
            "noise": noise,
            "W4_words": W4_words,
            "W4_scales": W4_scales,
            "b4": b4,
            "W5_words": W5_words,
            "W5_scales": W5_scales,
            "b5": b5,
            "max_logvar": max_logvar,
            "min_logvar": min_logvar}


def reference(h3, state, noise, W4_words, W4_scales, b4, W5_words, W5_scales, b5, max_logvar, min_logvar):
    h4 = swish((mxq(f64(h3), 2, "e4m3") @ unpack_weight(W4_words, W4_scales, "e4m3").reshape(E, H, H)) + f64(b4)[:, None, :])
    out = (mxq(h4, 2, "e4m3") @ unpack_weight(W5_words, W5_scales, "e4m3").reshape(E, H, 2 * P)) + f64(b5)[:, None, :]
    mean = out[..., :P]
    logvar = out[..., P:]
    logvar = f64(max_logvar) - softplus(f64(max_logvar) - logvar)
    logvar = f64(min_logvar) + softplus(logvar - f64(min_logvar))
    stds = np.exp(0.5 * logvar)
    samples = mean + stds * f64(noise)
    delta_states = samples[..., :S]
    rewards = samples[..., S:]
    next_states = f64(state)[None] + delta_states
    return next_states, rewards

@@ -1,0 +1,388 @@
+from contextlib import ExitStack
+
+import concourse.mybir as mybir
+from concourse.masks import make_identity
+
+F32 = mybir.dt.float32
+BF16 = mybir.dt.bfloat16
+I32 = mybir.dt.int32
+U32 = mybir.dt.uint32
+U8 = mybir.dt.uint8
+FP8X4 = mybir.dt.float8_e4m3fn_x4
+ACT = mybir.ActivationFunctionType
+ALU = mybir.AluOpType
+
+E = 7
+B = 1024
+H = 512
+S = 127
+P = 128
+PACK = 4
+TILES = B // P
+PAIR = 2
+STEPS_PER_MEMBER = TILES // PAIR
+STEPS = E * STEPS_PER_MEMBER
+QUAD = 4
+UNITS_PER_MEMBER = TILES // QUAD
+UNITS = E * UNITS_PER_MEMBER
+LIVE_ROWS = 4
+
+FLOPS = 2 * E * B * H * (H + 2 * P)
+
+
+def tile_ensembledynamicsmodel_pa_e_kernel(
+    tc,
+    h3,
+    state,
+    noise,
+    W4_words,
+    W4_scales,
+    b4,
+    W5_words,
+    W5_scales,
+    b5,
+    max_logvar,
+    min_logvar,
+    out_0,
+    out_1,
+):
+    nc = tc.nc
+    with ExitStack() as ctx:
+        ctx.enter_context(tc.manual_schedule())
+        keep = ctx.enter_context(tc.tile_pool(name="keep", bufs=1))
+        work = ctx.enter_context(tc.tile_pool(name="work", bufs=2))
+        psum = ctx.enter_context(tc.psum_pool(name="psum", bufs=2))
+
+        ident_f32 = keep.tile([P, P], F32)
+        make_identity(nc, ident_f32[:])
+        ident_bf16 = keep.tile([P, P], BF16)
+        make_identity(nc, ident_bf16[:])
+
+        w4_scales = keep.tile([P, E, H], U8, align_bytes=64)
+        w5_scales = keep.tile([P, E, 2 * P], U8, align_bytes=64)
+        nc.vector.memset(w4_scales[:].rearrange("p e n -> p (e n)").bitcast(I32), 0)
+        nc.vector.memset(w5_scales[:].rearrange("p e n -> p (e n)").bitcast(I32), 0)
+        vector_rows = keep.tile([P, P], BF16)
+        nc.vector.memset(vector_rows[:], 0.0)
+
+        h3_sb = {}
+        w4_words = {}
+        w5_words = {}
+        b4_all = {}
+        noise_sb = {}
+
+        def load_h3(e, half):
+            rows = keep.tile([P, QUAD * H], BF16, name="h3_%d_%d" % (e, half))
+            by_partition = h3[e].rearrange("(p i) k -> p (i k)", i=TILES)
+            nc.sync.dma_start(out=rows[:], in_=by_partition[:, half * QUAD * H : (half + 1) * QUAD * H])
+            h3_sb[e, half] = rows
+
+        def load_words(words_in, e, columns, label):
+            words = keep.tile([P, columns], U32, name="%s_%d" % (label, e), align_bytes=64)
+            nc.sync.dma_start(
+                out=words[:].bitcast(I32),
+                in_=words_in[e].rearrange("p n t -> p (n t)").bitcast(I32),
+            )
+            return words
+
+        def load_scales(plane, scales_in):
+            for quadrant in range(P // 32):
+                first = quadrant * LIVE_ROWS
+                nc.sync.dma_start(
+                    out=plane[32 * quadrant : 32 * quadrant + LIVE_ROWS].bitcast(I32),
+                    in_=scales_in[:, first : first + LIVE_ROWS, :].rearrange("e r n -> r e n").bitcast(I32),
+                )
+
+        def load_b4(e):
+            spread = keep.tile([P, H], BF16, name="b4_%d" % e)
+            nc.sync.dma_start(out=spread[:], in_=b4[e].partition_broadcast(P))
+            b4_all[e] = spread
+
+        load_h3(0, 0)
+        load_scales(w4_scales, W4_scales)
+        w4_words[0] = load_words(W4_words, 0, H, "w4")
+        load_b4(0)
+        load_h3(0, 1)
+        nc.sync.dma_start(out=vector_rows[0:E, :], in_=b5[:, 0:P])
+        nc.sync.dma_start(out=vector_rows[E : 2 * E, :], in_=b5[:, P : 2 * P])
+        nc.sync.dma_start(out=vector_rows[2 * E : 2 * E + 1, :], in_=max_logvar)
+        nc.sync.dma_start(out=vector_rows[2 * E + 1 : 2 * E + 2, :], in_=min_logvar)
+        load_scales(w5_scales, W5_scales)
+        w5_words[0] = load_words(W5_words, 0, 2 * P, "w5")
+        for e in range(1, E):
+            load_h3(e, 0)
+            w4_words[e] = load_words(W4_words, e, H, "w4")
+            load_b4(e)
+            load_h3(e, 1)
+            w5_words[e] = load_words(W5_words, e, 2 * P, "w5")
+        state_sb = keep.tile([P, TILES, S], BF16)
+        nc.sync.dma_start(
+            out=state_sb[:].rearrange("p i s -> p (i s)"),
+            in_=state.rearrange("(p i) s -> p (i s)", i=TILES),
+        )
+        for e in range(E):
+            noise_e = keep.tile([P, TILES, P], BF16, name="noise_%d" % e)
+            nc.sync.dma_start(
+                out=noise_e[:].rearrange("p i c -> p (i c)"),
+                in_=noise[e].rearrange("(p i) c -> p (i c)", i=TILES),
+            )
+            noise_sb[e] = noise_e
+
+        h4_codes = {}
+        h4_scales = {}
+        tanh_sb = {}
+        for e in range(E):
+            h4_codes[e] = keep.tile([P, B], U32, name="h4_codes_%d" % e, align_bytes=64)
+            h4_scales[e] = keep.tile([P, B], U8, name="h4_scales_%d" % e, align_bytes=64)
+            tanh_sb[e] = keep.tile([P, B], F32, name="tanh_%d" % e)
+        rewards_sb = keep.tile([P, E, TILES, 1], F32)
+
+        vector_cols = keep.tile([P, 2 * E + 2], F32)
+        exps = keep.tile([P, 2], F32)
+        half_emax = keep.tile([P, 1], F32)
+        var_mid = keep.tile([P, 1], F32)
+        tanh_bias = keep.tile([P, E], F32)
+
+        def column_constants():
+            cols_ps = psum.tile([P, P], BF16, tag="tx")
+            nc.tensor.transpose(cols_ps[:], vector_rows[:], ident_bf16[:])
+            nc.vector.tensor_copy(out=vector_cols[:], in_=cols_ps[:, 0 : 2 * E + 2])
+            nc.scalar.activation(out=exps[:], in_=vector_cols[:, 2 * E : 2 * E + 2], func=ACT.Exp)
+            nc.vector.tensor_scalar_mul(out=half_emax[:], in0=exps[:, 0:1], scalar1=0.5)
+            nc.vector.tensor_add(out=var_mid[:], in0=exps[:, 1:2], in1=half_emax[:])
+            nc.vector.tensor_scalar(
+                out=tanh_bias[:],
+                in0=vector_cols[:, E : 2 * E],
+                scalar1=vector_cols[:, 2 * E : 2 * E + 1],
+                scalar2=0.5,
+                op0=ALU.subtract,
+                op1=ALU.mult,
+            )
+
+        live = {}
+
+        def member_of(s):
+            return s // STEPS_PER_MEMBER
+
+        def columns_of(s):
+            pair = s % STEPS_PER_MEMBER
+            return slice(pair * PAIR * P, (pair + 1) * PAIR * P)
+
+        def transpose_h3(s):
+            e, pair = divmod(s, STEPS_PER_MEMBER)
+            words = h3_sb[e, pair * PAIR // QUAD][:].bitcast(F32)
+            xt = psum.tile([P, PAIR, 2, P], F32, tag="tx")
+            for i in range(PAIR):
+                first = ((pair * PAIR + i) % QUAD) * (H // 2)
+                for u in range(2):
+                    nc.tensor.transpose(xt[:, i, u, :], words[:, first + u : first + H // 2 : 2], ident_f32[:])
+            live["xt", s] = xt
+
+        def copy_h3(s):
+            grouped = work.tile([P, PAIR * P * PACK], BF16, tag="h3_grouped", align_bytes=64)
+            nc.scalar.copy(
+                out=grouped[:].bitcast(F32).rearrange("p (i b u) -> p i b u", i=PAIR, u=2),
+                in_=live["xt", s][:].rearrange("p i u b -> p i b u"),
+            )
+            live["h3_grouped", s] = grouped
+
+        def quantise_h3(s):
+            codes = work.tile([P, PAIR * P], U32, tag="h3_codes", align_bytes=64)
+            scales = work.tile([P, PAIR * P], U8, tag="h3_scales", align_bytes=64)
+            nc.vector.quantize_mx(out=codes[:].bitcast(FP8X4), scales=scales[:], in_=live["h3_grouped", s][:])
+            live["h3_mx", s] = (codes, scales)
+
+        def layer4(s):
+            e = member_of(s)
+            codes, scales = live["h3_mx", s]
+            for i in range(PAIR):
+                acc = psum.tile([P, H], F32, tag="ta")
+                nc.tensor.matmul_mx(
+                    out=acc[:],
+                    lhsT=codes[:, i * P : (i + 1) * P].bitcast(FP8X4),
+                    lhsT_scale=scales[:, i * P : (i + 1) * P],
+                    rhs=w4_words[e][:].bitcast(FP8X4),
+                    rhs_scale=w4_scales[:, e, :],
+                    start=True,
+                    stop=True,
+                )
+                live["acc", s, i] = acc
+
+        def add_b4(s):
+            e = member_of(s)
+            for i in range(PAIR):
+                z = work.tile([P, PACK, P], F32, tag="z", bufs=2 * PAIR)
+                nc.vector.tensor_tensor(
+                    out=z[:],
+                    in0=live["acc", s, i][:].rearrange("p (c t) -> p t c", t=PACK),
+                    in1=b4_all[e][:].rearrange("p (c t) -> p t c", t=PACK),
+                    op=ALU.add,
+                )
+                live["z", s, i] = z
+
+        def transpose_z(s):
+            for i in range(PAIR):
+                z = live["z", s, i]
+                zt = psum.tile([P, PACK, P], F32, tag="tz")
+                for t in range(PACK):
+                    nc.tensor.transpose(zt[:, t, :], z[:, t, :], ident_f32[:])
+                live["zt", s, i] = zt
+
+        def swish(s):
+            grouped = work.tile([P, PAIR, P, PACK], BF16, tag="h4_grouped", align_bytes=64)
+            for i in range(PAIR):
+                nc.scalar.activation(
+                    out=grouped[:, i],
+                    in_=live["zt", s, i][:].rearrange("p t b -> p b t"),
+                    func=ACT.Silu,
+                )
+            live["h4_grouped", s] = grouped
+
+        def quantise_h4(s):
+            e, cols = member_of(s), columns_of(s)
+            nc.vector.quantize_mx(
+                out=h4_codes[e][:, cols].bitcast(FP8X4),
+                scales=h4_scales[e][:, cols],
+                in_=live["h4_grouped", s][:].rearrange("p i b t -> p (i b t)"),
+            )
+
+        def logvar(s):
+            e, cols = member_of(s), columns_of(s)
+            lv = psum.tile([P, PAIR * P], F32, tag="tl")
+            nc.tensor.matmul_mx(
+                out=lv[:],
+                lhsT=w5_words[e][:, P : 2 * P].bitcast(FP8X4),
+                lhsT_scale=w5_scales[:, e, P : 2 * P],
+                rhs=h4_codes[e][:, cols].bitcast(FP8X4),
+                rhs_scale=h4_scales[e][:, cols],
+                start=True,
+                stop=True,
+            )
+            live["lv", s] = lv
+
+        def clamp_tanh(s):
+            e, cols = member_of(s), columns_of(s)
+            nc.scalar.activation(
+                out=tanh_sb[e][:, cols],
+                in_=live["lv", s][:],
+                func=ACT.Tanh,
+                bias=tanh_bias[:, e : e + 1],
+                scale=0.5,
+            )
+
+        def stage(function, s):
+            if 0 <= s < STEPS:
+                function(s)
+
+        def first_part_round(r):
+            stage(transpose_h3, r + 2)
+            stage(transpose_z, r)
+            stage(copy_h3, r + 2)
+            stage(swish, r)
+            stage(layer4, r + 1)
+            stage(logvar, r - 1)
+            stage(quantise_h3, r + 2)
+            stage(add_b4, r + 1)
+            stage(quantise_h4, r)
+            stage(clamp_tanh, r - 1)
+
+        first_part_round(-2)
+        first_part_round(-1)
+        column_constants()
+        for r in range(STEPS + 1):
+            first_part_round(r)
+
+        def unit_columns(u):
+            half = u % UNITS_PER_MEMBER
+            return slice(half * QUAD * P, (half + 1) * QUAD * P)
+
+        def stds(u):
+            e, cols = u // UNITS_PER_MEMBER, unit_columns(u)
+            std = work.tile([P, QUAD * P], F32, tag="std", bufs=4)
+            nc.scalar.activation(
+                out=std[:], in_=tanh_sb[e][:, cols], func=ACT.Sqrt, bias=var_mid[:], scale=half_emax[:]
+            )
+            live["std", u] = std
+
+        def transpose_noise(u):
+            e, half = divmod(u, UNITS_PER_MEMBER)
+            noise_t = psum.tile([P, QUAD, P], BF16, tag="tx")
+            for j in range(QUAD):
+                nc.tensor.transpose(noise_t[:, j, :], noise_sb[e][:, half * QUAD + j, :], ident_bf16[:])
+            live["noise_t", u] = noise_t
+
+        def mean(u):
+            e, cols = u // UNITS_PER_MEMBER, unit_columns(u)
+            mean_ps = psum.tile([P, QUAD * P], F32, tag="ta")
+            nc.tensor.matmul_mx(
+                out=mean_ps[:],
+                lhsT=w5_words[e][:, 0:P].bitcast(FP8X4),
+                lhsT_scale=w5_scales[:, e, 0:P],
+                rhs=h4_codes[e][:, cols].bitcast(FP8X4),
+                rhs_scale=h4_scales[e][:, cols],
+                start=True,
+                stop=True,
+            )
+            live["mean", u] = mean_ps
+
+        def sample(u):
+            e = u // UNITS_PER_MEMBER
+            spread = work.tile([P, QUAD * P], F32, tag="spread")
+            nc.vector.tensor_tensor(
+                out=spread[:],
+                in0=live["noise_t", u][:].rearrange("p j b -> p (j b)"),
+                in1=live["std", u][:],
+                op=ALU.mult,
+            )
+            samples = work.tile([P, QUAD * P], F32, tag="samples")
+            nc.vector.scalar_tensor_tensor(
+                out=samples[:],
+                in0=live["mean", u][:],
+                scalar=vector_cols[:, e : e + 1],
+                in1=spread[:],
+                op0=ALU.add,
+                op1=ALU.add,
+            )
+            live["samples", u] = samples
+
+        def transpose_back(u):
+            samples = live["samples", u]
+            back = psum.tile([P, QUAD, P], F32, tag="tz")
+            for j in range(QUAD):
+                nc.tensor.transpose(back[:, j, :], samples[:, j * P : (j + 1) * P], ident_f32[:])
+            live["back", u] = back
+
+        def finish(u):
+            e, half = divmod(u, UNITS_PER_MEMBER)
+            tiles = slice(half * QUAD, (half + 1) * QUAD)
+            if half == 0:
+                next_states = work.tile([P, TILES, S], F32, tag="next_states")
+                live["next_states", e] = next_states
+            next_states = live["next_states", e]
+            back = live["back", u]
+            nc.vector.tensor_tensor(
+                out=next_states[:, tiles, :], in0=back[:, :, 0:S], in1=state_sb[:, tiles, :], op=ALU.add
+            )
+            nc.vector.tensor_copy(out=rewards_sb[:, e, tiles, :], in_=back[:, :, S : S + 1])
+            if half == UNITS_PER_MEMBER - 1:
+                nc.sync.dma_start(
+                    out=out_0[e].rearrange("(p i) s -> p (i s)", i=TILES),
+                    in_=next_states[:].rearrange("p i s -> p (i s)"),
+                )
+
+        def unit_stage(function, u):
+            if 0 <= u < UNITS:
+                function(u)
+
+        for r in range(-1, UNITS):
+            unit_stage(stds, r + 1)
+            unit_stage(transpose_noise, r + 1)
+            unit_stage(mean, r + 1)
+            unit_stage(transpose_back, r)
+            unit_stage(sample, r + 1)
+            unit_stage(finish, r)
+
+        nc.sync.dma_start(
+            out=out_1.rearrange("e (p i) o -> p e (i o)", i=TILES),
+            in_=rewards_sb[:].rearrange("p e i o -> p e (i o)"),
+        )

@@ -23,8 +23,7 @@ PAIR = 2
 STEPS_PER_MEMBER = TILES // PAIR
 STEPS = E * STEPS_PER_MEMBER
 QUAD = 4
-UNITS_PER_MEMBER = TILES // QUAD
-UNITS = E * UNITS_PER_MEMBER
+HALVES = TILES // QUAD
 LIVE_ROWS = 4
 
 FLOPS = 2 * E * B * H * (H + 2 * P)
@@ -93,10 +92,18 @@ def tile_ensembledynamicsmodel_pa_e_kernel(
                     in_=scales_in[:, first : first + LIVE_ROWS, :].rearrange("e r n -> r e n").bitcast(I32),
                 )
 
+        def load_noise(e):
+            rows = keep.tile([P, TILES, P], BF16, name="noise_%d" % e)
+            nc.sync.dma_start(
+                out=rows[:].rearrange("p i c -> p (i c)"),
+                in_=noise[e].rearrange("(p i) c -> p (i c)", i=TILES),
+            )
+            noise_sb[e] = rows
+
         def load_b4(e):
-            spread = keep.tile([P, H], BF16, name="b4_%d" % e)
-            nc.sync.dma_start(out=spread[:], in_=b4[e].partition_broadcast(P))
-            b4_all[e] = spread
+            copies = keep.tile([P, H], BF16, name="b4_%d" % e)
+            nc.sync.dma_start(out=copies[:], in_=b4[e].partition_broadcast(P))
+            b4_all[e] = copies
 
         load_h3(0, 0)
         load_scales(w4_scales, W4_scales)
@@ -109,32 +116,29 @@ def tile_ensembledynamicsmodel_pa_e_kernel(
         nc.sync.dma_start(out=vector_rows[2 * E + 1 : 2 * E + 2, :], in_=min_logvar)
         load_scales(w5_scales, W5_scales)
         w5_words[0] = load_words(W5_words, 0, 2 * P, "w5")
+        load_noise(0)
         for e in range(1, E):
             load_h3(e, 0)
             w4_words[e] = load_words(W4_words, e, H, "w4")
             load_b4(e)
             load_h3(e, 1)
             w5_words[e] = load_words(W5_words, e, 2 * P, "w5")
+            load_noise(e)
         state_sb = keep.tile([P, TILES, S], BF16)
         nc.sync.dma_start(
             out=state_sb[:].rearrange("p i s -> p (i s)"),
             in_=state.rearrange("(p i) s -> p (i s)", i=TILES),
         )
-        for e in range(E):
-            noise_e = keep.tile([P, TILES, P], BF16, name="noise_%d" % e)
-            nc.sync.dma_start(
-                out=noise_e[:].rearrange("p i c -> p (i c)"),
-                in_=noise[e].rearrange("(p i) c -> p (i c)", i=TILES),
-            )
-            noise_sb[e] = noise_e
 
         h4_codes = {}
         h4_scales = {}
-        tanh_sb = {}
+        clamped = {}
+        noise_t = {}
         for e in range(E):
             h4_codes[e] = keep.tile([P, B], U32, name="h4_codes_%d" % e, align_bytes=64)
             h4_scales[e] = keep.tile([P, B], U8, name="h4_scales_%d" % e, align_bytes=64)
-            tanh_sb[e] = keep.tile([P, B], F32, name="tanh_%d" % e)
+            clamped[e] = keep.tile([P, B], F32, name="clamped_%d" % e)
+            noise_t[e] = keep.tile([P, B], BF16, name="noise_t_%d" % e)
         rewards_sb = keep.tile([P, E, TILES, 1], F32)
 
         vector_cols = keep.tile([P, 2 * E + 2], F32)
@@ -248,7 +252,7 @@ def tile_ensembledynamicsmodel_pa_e_kernel(
 
         def logvar(s):
             e, cols = member_of(s), columns_of(s)
-            lv = psum.tile([P, PAIR * P], F32, tag="tl")
+            lv = psum.tile([P, PAIR * P], F32, tag="tl", bufs=1)
             nc.tensor.matmul_mx(
                 out=lv[:],
                 lhsT=w5_words[e][:, P : 2 * P].bitcast(FP8X4),
@@ -263,12 +267,29 @@ def tile_ensembledynamicsmodel_pa_e_kernel(
         def clamp_tanh(s):
             e, cols = member_of(s), columns_of(s)
             nc.scalar.activation(
-                out=tanh_sb[e][:, cols],
+                out=clamped[e][:, cols],
                 in_=live["lv", s][:],
                 func=ACT.Tanh,
                 bias=tanh_bias[:, e : e + 1],
                 scale=0.5,
             )
+
+        def transpose_noise(s):
+            e, pair = divmod(s, STEPS_PER_MEMBER)
+            noise_ps = psum.tile([P, PAIR, P], F32, tag="tn", bufs=1)
+            for i in range(PAIR):
+                nc.tensor.matmul(
+                    out=noise_ps[:, i, :],
+                    lhsT=noise_sb[e][:, pair * PAIR + i, :],
+                    rhs=ident_bf16[:],
+                    start=True,
+                    stop=True,
+                )
+            live["noise_ps", s] = noise_ps
+
+        def copy_noise(s):
+            e, cols = member_of(s), columns_of(s)
+            nc.vector.tensor_copy(out=noise_t[e][:, cols], in_=live["noise_ps", s][:].rearrange("p i b -> p (i b)"))
 
         def stage(function, s):
             if 0 <= s < STEPS:
@@ -281,9 +302,11 @@ def tile_ensembledynamicsmodel_pa_e_kernel(
             stage(swish, r)
             stage(layer4, r + 1)
             stage(logvar, r - 1)
+            stage(transpose_noise, r - 1)
             stage(quantise_h3, r + 2)
             stage(add_b4, r + 1)
             stage(quantise_h4, r)
+            stage(copy_noise, r - 1)
             stage(clamp_tanh, r - 1)
 
         first_part_round(-2)
@@ -292,95 +315,88 @@ def tile_ensembledynamicsmodel_pa_e_kernel(
         for r in range(STEPS + 1):
             first_part_round(r)
 
-        def unit_columns(u):
-            half = u % UNITS_PER_MEMBER
+        def half_columns(half):
             return slice(half * QUAD * P, (half + 1) * QUAD * P)
 
-        def stds(u):
-            e, cols = u // UNITS_PER_MEMBER, unit_columns(u)
-            std = work.tile([P, QUAD * P], F32, tag="std", bufs=4)
-            nc.scalar.activation(
-                out=std[:], in_=tanh_sb[e][:, cols], func=ACT.Sqrt, bias=var_mid[:], scale=half_emax[:]
-            )
-            live["std", u] = std
-
-        def transpose_noise(u):
-            e, half = divmod(u, UNITS_PER_MEMBER)
-            noise_t = psum.tile([P, QUAD, P], BF16, tag="tx")
-            for j in range(QUAD):
-                nc.tensor.transpose(noise_t[:, j, :], noise_sb[e][:, half * QUAD + j, :], ident_bf16[:])
-            live["noise_t", u] = noise_t
-
-        def mean(u):
-            e, cols = u // UNITS_PER_MEMBER, unit_columns(u)
-            mean_ps = psum.tile([P, QUAD * P], F32, tag="ta")
-            nc.tensor.matmul_mx(
-                out=mean_ps[:],
-                lhsT=w5_words[e][:, 0:P].bitcast(FP8X4),
-                lhsT_scale=w5_scales[:, e, 0:P],
-                rhs=h4_codes[e][:, cols].bitcast(FP8X4),
-                rhs_scale=h4_scales[e][:, cols],
-                start=True,
-                stop=True,
-            )
-            live["mean", u] = mean_ps
-
-        def sample(u):
-            e = u // UNITS_PER_MEMBER
-            spread = work.tile([P, QUAD * P], F32, tag="spread")
-            nc.vector.tensor_tensor(
-                out=spread[:],
-                in0=live["noise_t", u][:].rearrange("p j b -> p (j b)"),
-                in1=live["std", u][:],
-                op=ALU.mult,
-            )
-            samples = work.tile([P, QUAD * P], F32, tag="samples")
-            nc.vector.scalar_tensor_tensor(
-                out=samples[:],
-                in0=live["mean", u][:],
-                scalar=vector_cols[:, e : e + 1],
-                in1=spread[:],
-                op0=ALU.add,
-                op1=ALU.add,
-            )
-            live["samples", u] = samples
-
-        def transpose_back(u):
-            samples = live["samples", u]
-            back = psum.tile([P, QUAD, P], F32, tag="tz")
-            for j in range(QUAD):
-                nc.tensor.transpose(back[:, j, :], samples[:, j * P : (j + 1) * P], ident_f32[:])
-            live["back", u] = back
-
-        def finish(u):
-            e, half = divmod(u, UNITS_PER_MEMBER)
-            tiles = slice(half * QUAD, (half + 1) * QUAD)
-            if half == 0:
-                next_states = work.tile([P, TILES, S], F32, tag="next_states")
-                live["next_states", e] = next_states
-            next_states = live["next_states", e]
-            back = live["back", u]
-            nc.vector.tensor_tensor(
-                out=next_states[:, tiles, :], in0=back[:, :, 0:S], in1=state_sb[:, tiles, :], op=ALU.add
-            )
-            nc.vector.tensor_copy(out=rewards_sb[:, e, tiles, :], in_=back[:, :, S : S + 1])
-            if half == UNITS_PER_MEMBER - 1:
-                nc.sync.dma_start(
-                    out=out_0[e].rearrange("(p i) s -> p (i s)", i=TILES),
-                    in_=next_states[:].rearrange("p i s -> p (i s)"),
+        def stds(e):
+            for half in range(HALVES):
+                cols = half_columns(half)
+                nc.scalar.activation(
+                    out=clamped[e][:, cols],
+                    in_=clamped[e][:, cols],
+                    func=ACT.Sqrt,
+                    bias=var_mid[:],
+                    scale=half_emax[:],
                 )
 
-        def unit_stage(function, u):
-            if 0 <= u < UNITS:
-                function(u)
+        def spread_noise(e):
+            for half in range(HALVES):
+                cols = half_columns(half)
+                spread = work.tile([P, QUAD * P], F32, tag="spread", bufs=2 * HALVES)
+                nc.gpsimd.tensor_tensor(out=spread[:], in0=clamped[e][:, cols], in1=noise_t[e][:, cols], op=ALU.mult)
+                live["spread", e, half] = spread
 
-        for r in range(-1, UNITS):
-            unit_stage(stds, r + 1)
-            unit_stage(transpose_noise, r + 1)
-            unit_stage(mean, r + 1)
-            unit_stage(transpose_back, r)
-            unit_stage(sample, r + 1)
-            unit_stage(finish, r)
+        def mean(e):
+            for half in range(HALVES):
+                cols = half_columns(half)
+                mean_ps = psum.tile([P, QUAD * P], F32, tag="ta")
+                nc.tensor.matmul_mx(
+                    out=mean_ps[:],
+                    lhsT=w5_words[e][:, 0:P].bitcast(FP8X4),
+                    lhsT_scale=w5_scales[:, e, 0:P],
+                    rhs=h4_codes[e][:, cols].bitcast(FP8X4),
+                    rhs_scale=h4_scales[e][:, cols],
+                    start=True,
+                    stop=True,
+                )
+                live["mean", e, half] = mean_ps
+
+        def sample(e):
+            for half in range(HALVES):
+                samples = work.tile([P, QUAD * P], F32, tag="samples", bufs=2 * HALVES)
+                nc.vector.scalar_tensor_tensor(
+                    out=samples[:],
+                    in0=live["mean", e, half][:],
+                    scalar=vector_cols[:, e : e + 1],
+                    in1=live["spread", e, half][:],
+                    op0=ALU.add,
+                    op1=ALU.add,
+                )
+                live["samples", e, half] = samples
+
+        def transpose_back(e):
+            for half in range(HALVES):
+                samples = live["samples", e, half]
+                back = psum.tile([P, QUAD, P], F32, tag="tz")
+                for j in range(QUAD):
+                    nc.tensor.transpose(back[:, j, :], samples[:, j * P : (j + 1) * P], ident_f32[:])
+                live["back", e, half] = back
+
+        def finish(e):
+            next_states = work.tile([P, TILES, S], F32, tag="next_states")
+            for half in range(HALVES):
+                tiles = slice(half * QUAD, (half + 1) * QUAD)
+                back = live["back", e, half]
+                nc.vector.tensor_tensor(
+                    out=next_states[:, tiles, :], in0=back[:, :, 0:S], in1=state_sb[:, tiles, :], op=ALU.add
+                )
+                nc.vector.tensor_copy(out=rewards_sb[:, e, tiles, :], in_=back[:, :, S : S + 1])
+            nc.sync.dma_start(
+                out=out_0[e].rearrange("(p i) s -> p (i s)", i=TILES),
+                in_=next_states[:].rearrange("p i s -> p (i s)"),
+            )
+
+        def member_stage(function, e):
+            if 0 <= e < E:
+                function(e)
+
+        for r in range(-2, E):
+            member_stage(mean, r + 1)
+            member_stage(transpose_back, r)
+            member_stage(sample, r + 1)
+            member_stage(finish, r)
+            member_stage(stds, r + 2)
+            member_stage(spread_noise, r + 2)
 
         nc.sync.dma_start(
             out=out_1.rearrange("e (p i) o -> p e (i o)", i=TILES),

@@ -215,7 +215,7 @@ def tile_ensembledynamicsmodel_pa_e_kernel(
         def add_b4(s):
             e = member_of(s)
             for i in range(PAIR):
-                z = work.tile([P, PACK, P], F32, tag="z", bufs=2 * PAIR)
+                z = work.tile([P, PACK, P], F32, tag="z", bufs=3 * PAIR)
                 nc.vector.tensor_tensor(
                     out=z[:],
                     in0=live["acc", s, i][:].rearrange("p (c t) -> p t c", t=PACK),
@@ -297,22 +297,22 @@ def tile_ensembledynamicsmodel_pa_e_kernel(
 
         def first_part_round(r):
             stage(transpose_h3, r + 2)
-            stage(transpose_z, r)
+            stage(transpose_z, r - 1)
             stage(copy_h3, r + 2)
-            stage(swish, r)
+            stage(swish, r - 1)
             stage(layer4, r + 1)
-            stage(logvar, r - 1)
-            stage(transpose_noise, r - 1)
+            stage(logvar, r - 2)
+            stage(transpose_noise, r - 2)
             stage(quantise_h3, r + 2)
             stage(add_b4, r + 1)
-            stage(quantise_h4, r)
-            stage(copy_noise, r - 1)
-            stage(clamp_tanh, r - 1)
+            stage(quantise_h4, r - 1)
+            stage(copy_noise, r - 2)
+            stage(clamp_tanh, r - 2)
 
         first_part_round(-2)
         first_part_round(-1)
         column_constants()
-        for r in range(STEPS + 1):
+        for r in range(STEPS + 2):
             first_part_round(r)
 
         def half_columns(half):

@@ -20,11 +20,12 @@ P = 128
 PACK = 4
 TILES = B // P
 PAIR = 2
-STEPS_PER_MEMBER = TILES // PAIR
-STEPS = E * STEPS_PER_MEMBER
 QUAD = 4
 HALVES = TILES // QUAD
+STEPS = E * HALVES
+N = QUAD * P
 LIVE_ROWS = 4
+GROUP = 4
 
 FLOPS = 2 * E * B * H * (H + 2 * P)
 
@@ -50,30 +51,39 @@ def tile_ensembledynamicsmodel_pa_e_kernel(
         ctx.enter_context(tc.manual_schedule())
         keep = ctx.enter_context(tc.tile_pool(name="keep", bufs=1))
         work = ctx.enter_context(tc.tile_pool(name="work", bufs=2))
-        psum = ctx.enter_context(tc.psum_pool(name="psum", bufs=2))
+        psum = ctx.enter_context(tc.psum_pool(name="psum", bufs=1))
 
         ident_f32 = keep.tile([P, P], F32)
         make_identity(nc, ident_f32[:])
         ident_bf16 = keep.tile([P, P], BF16)
         make_identity(nc, ident_bf16[:])
 
-        w4_scales = keep.tile([P, E, H], U8, align_bytes=64)
-        w5_scales = keep.tile([P, E, 2 * P], U8, align_bytes=64)
-        nc.vector.memset(w4_scales[:].rearrange("p e n -> p (e n)").bitcast(I32), 0)
-        nc.vector.memset(w5_scales[:].rearrange("p e n -> p (e n)").bitcast(I32), 0)
+        groups = (E + GROUP - 1) // GROUP
+        w4_scales_raw = keep.tile([P, groups, H], U8, align_bytes=64)
+        w4_scales = keep.tile([P, groups, PACK, P], U8, align_bytes=64)
+        w5_scales = keep.tile([P, groups, 2 * P], U8, align_bytes=64)
+        nc.vector.memset(w4_scales_raw[:].rearrange("p g n -> p (g n)").bitcast(I32), 0)
+        b4_rows = keep.tile([P, H], BF16)
+        nc.vector.memset(b4_rows[:], 0.0)
         vector_rows = keep.tile([P, P], BF16)
         nc.vector.memset(vector_rows[:], 0.0)
+        nc.vector.memset(w5_scales[:].rearrange("p g n -> p (g n)").bitcast(I32), 0)
 
         h3_sb = {}
+        w4_loaded = {}
         w4_words = {}
         w5_words = {}
-        b4_all = {}
         noise_sb = {}
 
-        def load_h3(e, half):
+        def load_h3(e, half, pieces=1):
             rows = keep.tile([P, QUAD * H], BF16, name="h3_%d_%d" % (e, half))
             by_partition = h3[e].rearrange("(p i) k -> p (i k)", i=TILES)
-            nc.sync.dma_start(out=rows[:], in_=by_partition[:, half * QUAD * H : (half + 1) * QUAD * H])
+            width = QUAD * H // pieces
+            for piece in range(pieces):
+                first = half * QUAD * H + piece * width
+                nc.sync.dma_start(
+                    out=rows[:, piece * width : (piece + 1) * width], in_=by_partition[:, first : first + width]
+                )
             h3_sb[e, half] = rows
 
         def load_words(words_in, e, columns, label):
@@ -84,12 +94,15 @@ def tile_ensembledynamicsmodel_pa_e_kernel(
             )
             return words
 
-        def load_scales(plane, scales_in):
+        def load_scales(plane, scales_in, group):
+            members = min(GROUP, E - group * GROUP)
             for quadrant in range(P // 32):
                 first = quadrant * LIVE_ROWS
                 nc.sync.dma_start(
-                    out=plane[32 * quadrant : 32 * quadrant + LIVE_ROWS].bitcast(I32),
-                    in_=scales_in[:, first : first + LIVE_ROWS, :].rearrange("e r n -> r e n").bitcast(I32),
+                    out=plane[32 * quadrant : 32 * quadrant + members * LIVE_ROWS, group, :].bitcast(I32),
+                    in_=scales_in[
+                        group * GROUP : group * GROUP + members, first : first + LIVE_ROWS, :
+                    ].bitcast(I32),
                 )
 
         def load_noise(e):
@@ -100,27 +113,24 @@ def tile_ensembledynamicsmodel_pa_e_kernel(
             )
             noise_sb[e] = rows
 
-        def load_b4(e):
-            copies = keep.tile([P, H], BF16, name="b4_%d" % e)
-            nc.sync.dma_start(out=copies[:], in_=b4[e].partition_broadcast(P))
-            b4_all[e] = copies
-
-        load_h3(0, 0)
-        load_scales(w4_scales, W4_scales)
-        w4_words[0] = load_words(W4_words, 0, H, "w4")
-        load_b4(0)
-        load_h3(0, 1)
+        load_h3(0, 0, PAIR)
+        w4_loaded[0] = load_words(W4_words, 0, H, "w4_loaded")
+        load_scales(w4_scales_raw, W4_scales, 0)
+        nc.sync.dma_start(out=b4_rows[0:E, :], in_=b4)
         nc.sync.dma_start(out=vector_rows[0:E, :], in_=b5[:, 0:P])
         nc.sync.dma_start(out=vector_rows[E : 2 * E, :], in_=b5[:, P : 2 * P])
         nc.sync.dma_start(out=vector_rows[2 * E : 2 * E + 1, :], in_=max_logvar)
         nc.sync.dma_start(out=vector_rows[2 * E + 1 : 2 * E + 2, :], in_=min_logvar)
-        load_scales(w5_scales, W5_scales)
+        load_h3(0, 1)
+        load_scales(w5_scales, W5_scales, 0)
         w5_words[0] = load_words(W5_words, 0, 2 * P, "w5")
         load_noise(0)
         for e in range(1, E):
             load_h3(e, 0)
-            w4_words[e] = load_words(W4_words, e, H, "w4")
-            load_b4(e)
+            w4_loaded[e] = load_words(W4_words, e, H, "w4_loaded")
+            if e % GROUP == 0:
+                load_scales(w4_scales_raw, W4_scales, e // GROUP)
+                load_scales(w5_scales, W5_scales, e // GROUP)
             load_h3(e, 1)
             w5_words[e] = load_words(W5_words, e, 2 * P, "w5")
             load_noise(e)
@@ -141,6 +151,7 @@ def tile_ensembledynamicsmodel_pa_e_kernel(
             noise_t[e] = keep.tile([P, B], BF16, name="noise_t_%d" % e)
         rewards_sb = keep.tile([P, E, TILES, 1], F32)
 
+        b4_cols = keep.tile([P, PACK, E], F32)
         vector_cols = keep.tile([P, 2 * E + 2], F32)
         exps = keep.tile([P, 2], F32)
         half_emax = keep.tile([P, 1], F32)
@@ -148,8 +159,12 @@ def tile_ensembledynamicsmodel_pa_e_kernel(
         tanh_bias = keep.tile([P, E], F32)
 
         def column_constants():
-            cols_ps = psum.tile([P, P], BF16, tag="tx")
+            b4_ps = psum.tile([P, PACK, P], BF16, tag="tn")
+            for t in range(PACK):
+                nc.tensor.transpose(b4_ps[:, t, :], b4_rows[:, t::PACK], ident_bf16[:])
+            cols_ps = psum.tile([P, P], BF16, tag="tl")
             nc.tensor.transpose(cols_ps[:], vector_rows[:], ident_bf16[:])
+            nc.vector.tensor_copy(out=b4_cols[:], in_=b4_ps[:, :, 0:E])
             nc.vector.tensor_copy(out=vector_cols[:], in_=cols_ps[:, 0 : 2 * E + 2])
             nc.scalar.activation(out=exps[:], in_=vector_cols[:, 2 * E : 2 * E + 2], func=ACT.Exp)
             nc.vector.tensor_scalar_mul(out=half_emax[:], in0=exps[:, 0:1], scalar1=0.5)
@@ -163,83 +178,82 @@ def tile_ensembledynamicsmodel_pa_e_kernel(
                 op1=ALU.mult,
             )
 
+        def reorder_w4_scales(group):
+            nc.vector.tensor_copy(
+                out=w4_scales[:, group], in_=w4_scales_raw[:, group, :].rearrange("p (m t) -> p t m", t=PACK)
+            )
+
+        def reorder_w4(e):
+            words = keep.tile([P, PACK, P], U32, name="w4_%d" % e, align_bytes=64)
+            nc.vector.tensor_copy(
+                out=words[:].bitcast(I32),
+                in_=w4_loaded[e][:].bitcast(I32).rearrange("p (m t) -> p t m", t=PACK),
+            )
+            w4_words[e] = words
+
         live = {}
 
         def member_of(s):
-            return s // STEPS_PER_MEMBER
+            return s // HALVES
 
         def columns_of(s):
-            pair = s % STEPS_PER_MEMBER
-            return slice(pair * PAIR * P, (pair + 1) * PAIR * P)
+            half = s % HALVES
+            return slice(half * N, (half + 1) * N)
 
-        def transpose_h3(s):
-            e, pair = divmod(s, STEPS_PER_MEMBER)
-            words = h3_sb[e, pair * PAIR // QUAD][:].bitcast(F32)
-            xt = psum.tile([P, PAIR, 2, P], F32, tag="tx")
+        def transpose_h3(s, pair):
+            words = h3_sb[divmod(s, HALVES)][:].bitcast(F32)
+            xt = psum.tile([P, PAIR, 2, P], F32, tag="tx", bufs=2)
             for i in range(PAIR):
-                first = ((pair * PAIR + i) % QUAD) * (H // 2)
+                first = (pair * PAIR + i) * (H // 2)
                 for u in range(2):
                     nc.tensor.transpose(xt[:, i, u, :], words[:, first + u : first + H // 2 : 2], ident_f32[:])
-            live["xt", s] = xt
+            live["xt", s, pair] = xt
 
-        def copy_h3(s):
-            grouped = work.tile([P, PAIR * P * PACK], BF16, tag="h3_grouped", align_bytes=64)
-            nc.scalar.copy(
-                out=grouped[:].bitcast(F32).rearrange("p (i b u) -> p i b u", i=PAIR, u=2),
-                in_=live["xt", s][:].rearrange("p i u b -> p i b u"),
+        def copy_h3(copy, s, pair):
+            if pair == 0:
+                live["h3_grouped", s] = work.tile([P, N * PACK], BF16, tag="h3_grouped", name="h3_grouped", align_bytes=64)
+            width = PAIR * P * PACK
+            copy(
+                out=live["h3_grouped", s][:, pair * width : (pair + 1) * width]
+                .bitcast(F32)
+                .rearrange("p (i b u) -> p i b u", i=PAIR, u=2),
+                in_=live["xt", s, pair][:].rearrange("p i u b -> p i b u"),
             )
-            live["h3_grouped", s] = grouped
 
         def quantise_h3(s):
-            codes = work.tile([P, PAIR * P], U32, tag="h3_codes", align_bytes=64)
-            scales = work.tile([P, PAIR * P], U8, tag="h3_scales", align_bytes=64)
+            codes = work.tile([P, N], U32, tag="h3_codes", align_bytes=64)
+            scales = work.tile([P, N], U8, tag="h3_scales", align_bytes=64)
             nc.vector.quantize_mx(out=codes[:].bitcast(FP8X4), scales=scales[:], in_=live["h3_grouped", s][:])
             live["h3_mx", s] = (codes, scales)
 
-        def layer4(s):
+        def layer4(s, t):
             e = member_of(s)
+            group, slot = divmod(e, GROUP)
             codes, scales = live["h3_mx", s]
-            for i in range(PAIR):
-                acc = psum.tile([P, H], F32, tag="ta")
-                nc.tensor.matmul_mx(
-                    out=acc[:],
-                    lhsT=codes[:, i * P : (i + 1) * P].bitcast(FP8X4),
-                    lhsT_scale=scales[:, i * P : (i + 1) * P],
-                    rhs=w4_words[e][:].bitcast(FP8X4),
-                    rhs_scale=w4_scales[:, e, :],
-                    start=True,
-                    stop=True,
-                )
-                live["acc", s, i] = acc
-
-        def add_b4(s):
-            e = member_of(s)
-            for i in range(PAIR):
-                z = work.tile([P, PACK, P], F32, tag="z", bufs=3 * PAIR)
-                nc.vector.tensor_tensor(
-                    out=z[:],
-                    in0=live["acc", s, i][:].rearrange("p (c t) -> p t c", t=PACK),
-                    in1=b4_all[e][:].rearrange("p (c t) -> p t c", t=PACK),
-                    op=ALU.add,
-                )
-                live["z", s, i] = z
-
-        def transpose_z(s):
-            for i in range(PAIR):
-                z = live["z", s, i]
-                zt = psum.tile([P, PACK, P], F32, tag="tz")
-                for t in range(PACK):
-                    nc.tensor.transpose(zt[:, t, :], z[:, t, :], ident_f32[:])
-                live["zt", s, i] = zt
+            acc = psum.tile([P, N], F32, tag="a%d" % t, name="acc")
+            nc.tensor.matmul_mx(
+                out=acc[:],
+                lhsT=w4_words[e][:, t, :].bitcast(FP8X4),
+                lhsT_scale=w4_scales[slot * LIVE_ROWS : P, group, t, :],
+                rhs=codes[:].bitcast(FP8X4),
+                rhs_scale=scales[:],
+                start=True,
+                stop=True,
+            )
+            live["acc", s, t] = acc
 
         def swish(s):
-            grouped = work.tile([P, PAIR, P, PACK], BF16, tag="h4_grouped", align_bytes=64)
-            for i in range(PAIR):
+            e = member_of(s)
+            h4 = work.tile([P, PACK, N], BF16, tag="h4")
+            for t in range(PACK):
                 nc.scalar.activation(
-                    out=grouped[:, i],
-                    in_=live["zt", s, i][:].rearrange("p t b -> p b t"),
-                    func=ACT.Silu,
+                    out=h4[:, t, :], in_=live["acc", s, t][:], func=ACT.Silu, bias=b4_cols[:, t, e : e + 1]
                 )
+            live["h4", s] = h4
+
+        def interleave_h4(s):
+            grouped = work.tile([P, N, PACK], BF16, tag="h4_grouped", align_bytes=64)
+            nc.vector.tensor_copy(out=grouped[:], in_=live["h4", s][:].rearrange("p t b -> p b t"))
             live["h4_grouped", s] = grouped
 
         def quantise_h4(s):
@@ -247,21 +261,24 @@ def tile_ensembledynamicsmodel_pa_e_kernel(
             nc.vector.quantize_mx(
                 out=h4_codes[e][:, cols].bitcast(FP8X4),
                 scales=h4_scales[e][:, cols],
-                in_=live["h4_grouped", s][:].rearrange("p i b t -> p (i b t)"),
+                in_=live["h4_grouped", s][:].rearrange("p b t -> p (b t)"),
             )
 
-        def logvar(s):
-            e, cols = member_of(s), columns_of(s)
-            lv = psum.tile([P, PAIR * P], F32, tag="tl", bufs=1)
+        def w5_pass(out, e, first, cols):
+            group, slot = divmod(e, GROUP)
             nc.tensor.matmul_mx(
-                out=lv[:],
-                lhsT=w5_words[e][:, P : 2 * P].bitcast(FP8X4),
-                lhsT_scale=w5_scales[:, e, P : 2 * P],
+                out=out,
+                lhsT=w5_words[e][:, first : first + P].bitcast(FP8X4),
+                lhsT_scale=w5_scales[slot * LIVE_ROWS : P, group, first : first + P],
                 rhs=h4_codes[e][:, cols].bitcast(FP8X4),
                 rhs_scale=h4_scales[e][:, cols],
                 start=True,
                 stop=True,
             )
+
+        def logvar(s):
+            lv = psum.tile([P, N], F32, tag="tl")
+            w5_pass(lv[:], member_of(s), P, columns_of(s))
             live["lv", s] = lv
 
         def clamp_tanh(s):
@@ -275,12 +292,12 @@ def tile_ensembledynamicsmodel_pa_e_kernel(
             )
 
         def transpose_noise(s):
-            e, pair = divmod(s, STEPS_PER_MEMBER)
-            noise_ps = psum.tile([P, PAIR, P], F32, tag="tn", bufs=1)
-            for i in range(PAIR):
+            e, half = divmod(s, HALVES)
+            noise_ps = psum.tile([P, QUAD, P], BF16, tag="tn")
+            for i in range(QUAD):
                 nc.tensor.matmul(
                     out=noise_ps[:, i, :],
-                    lhsT=noise_sb[e][:, pair * PAIR + i, :],
+                    lhsT=noise_sb[e][:, half * QUAD + i, :],
                     rhs=ident_bf16[:],
                     start=True,
                     stop=True,
@@ -291,74 +308,71 @@ def tile_ensembledynamicsmodel_pa_e_kernel(
             e, cols = member_of(s), columns_of(s)
             nc.vector.tensor_copy(out=noise_t[e][:, cols], in_=live["noise_ps", s][:].rearrange("p i b -> p (i b)"))
 
-        def stage(function, s):
+        def stage(function, s, *args):
             if 0 <= s < STEPS:
-                function(s)
+                function(s, *args)
 
         def first_part_round(r):
-            stage(transpose_h3, r + 2)
-            stage(transpose_z, r - 1)
-            stage(copy_h3, r + 2)
-            stage(swish, r - 1)
-            stage(layer4, r + 1)
-            stage(logvar, r - 2)
+            stage(layer4, r, 0)
+            stage(layer4, r, 1)
             stage(transpose_noise, r - 2)
-            stage(quantise_h3, r + 2)
-            stage(add_b4, r + 1)
-            stage(quantise_h4, r - 1)
-            stage(copy_noise, r - 2)
+            stage(transpose_h3, r + 2, 0)
+            stage(layer4, r, 2)
+            stage(layer4, r, 3)
+            stage(logvar, r - 2)
+            stage(transpose_h3, r + 2, 1)
+            stage(quantise_h3, r + 1)
+            if 0 <= r + 2 < STEPS:
+                copy_h3(nc.vector.tensor_copy, r + 2, 0)
+            stage(swish, r)
+            stage(interleave_h4, r - 1)
             stage(clamp_tanh, r - 2)
+            stage(copy_noise, r - 2)
+            if 0 <= r + 2 < STEPS:
+                copy_h3(nc.scalar.copy, r + 2, 1)
+            stage(quantise_h4, r - 1)
+            e, half = divmod(r + 2, HALVES)
+            if half == 0 and 0 < e < E:
+                reorder_w4(e)
+                if e % GROUP == 0:
+                    reorder_w4_scales(e // GROUP)
 
         first_part_round(-2)
-        first_part_round(-1)
         column_constants()
-        for r in range(STEPS + 2):
+        reorder_w4_scales(0)
+        reorder_w4(0)
+        for r in range(-1, STEPS + 2):
             first_part_round(r)
 
         def half_columns(half):
-            return slice(half * QUAD * P, (half + 1) * QUAD * P)
+            return slice(half * N, (half + 1) * N)
 
         def stds(e):
-            for half in range(HALVES):
-                cols = half_columns(half)
-                nc.scalar.activation(
-                    out=clamped[e][:, cols],
-                    in_=clamped[e][:, cols],
-                    func=ACT.Sqrt,
-                    bias=var_mid[:],
-                    scale=half_emax[:],
-                )
+            nc.scalar.activation(
+                out=clamped[e][:], in_=clamped[e][:], func=ACT.Sqrt, bias=var_mid[:], scale=half_emax[:]
+            )
 
         def spread_noise(e):
             for half in range(HALVES):
                 cols = half_columns(half)
-                spread = work.tile([P, QUAD * P], F32, tag="spread", bufs=2 * HALVES)
-                nc.gpsimd.tensor_tensor(out=spread[:], in0=clamped[e][:, cols], in1=noise_t[e][:, cols], op=ALU.mult)
-                live["spread", e, half] = spread
+                nc.gpsimd.tensor_tensor(
+                    out=clamped[e][:, cols], in0=clamped[e][:, cols], in1=noise_t[e][:, cols], op=ALU.mult
+                )
 
         def mean(e):
             for half in range(HALVES):
-                cols = half_columns(half)
-                mean_ps = psum.tile([P, QUAD * P], F32, tag="ta")
-                nc.tensor.matmul_mx(
-                    out=mean_ps[:],
-                    lhsT=w5_words[e][:, 0:P].bitcast(FP8X4),
-                    lhsT_scale=w5_scales[:, e, 0:P],
-                    rhs=h4_codes[e][:, cols].bitcast(FP8X4),
-                    rhs_scale=h4_scales[e][:, cols],
-                    start=True,
-                    stop=True,
-                )
+                mean_ps = psum.tile([P, N], F32, tag="a%d" % (e % 2 * HALVES + half), name="mean_ps")
+                w5_pass(mean_ps[:], e, 0, half_columns(half))
                 live["mean", e, half] = mean_ps
 
         def sample(e):
             for half in range(HALVES):
-                samples = work.tile([P, QUAD * P], F32, tag="samples", bufs=2 * HALVES)
+                samples = work.tile([P, N], F32, tag="samples", bufs=2 * HALVES)
                 nc.vector.scalar_tensor_tensor(
                     out=samples[:],
                     in0=live["mean", e, half][:],
                     scalar=vector_cols[:, e : e + 1],
-                    in1=live["spread", e, half][:],
+                    in1=clamped[e][:, half_columns(half)],
                     op0=ALU.add,
                     op1=ALU.add,
                 )
@@ -367,7 +381,7 @@ def tile_ensembledynamicsmodel_pa_e_kernel(
         def transpose_back(e):
             for half in range(HALVES):
                 samples = live["samples", e, half]
-                back = psum.tile([P, QUAD, P], F32, tag="tz")
+                back = psum.tile([P, QUAD, P], F32, tag="tx", bufs=2)
                 for j in range(QUAD):
                     nc.tensor.transpose(back[:, j, :], samples[:, j * P : (j + 1) * P], ident_f32[:])
                 live["back", e, half] = back

@@ -62,11 +62,14 @@ def tile_ensembledynamicsmodel_pa_e_kernel(
         w4_scales_raw = keep.tile([P, groups, H], U8, align_bytes=64)
         w4_scales = keep.tile([P, groups, PACK, P], U8, align_bytes=64)
         w5_scales = keep.tile([P, groups, 2 * P], U8, align_bytes=64)
-        nc.vector.memset(w4_scales_raw[:].rearrange("p g n -> p (g n)").bitcast(I32), 0)
+        warm = keep.tile([P, 1], F32)
+        nc.vector.memset(warm[:], 0.0)
+        nc.scalar.activation(out=warm[:], in_=warm[:], func=ACT.Exp)
         b4_rows = keep.tile([P, H], BF16)
         nc.vector.memset(b4_rows[:], 0.0)
         vector_rows = keep.tile([P, P], BF16)
         nc.vector.memset(vector_rows[:], 0.0)
+        nc.vector.memset(w4_scales_raw[:].rearrange("p g n -> p (g n)").bitcast(I32), 0)
         nc.vector.memset(w5_scales[:].rearrange("p g n -> p (g n)").bitcast(I32), 0)
 
         h3_sb = {}
@@ -113,14 +116,14 @@ def tile_ensembledynamicsmodel_pa_e_kernel(
             )
             noise_sb[e] = rows
 
+        nc.scalar.dma_start(out=b4_rows[0:E, :], in_=b4)
+        nc.scalar.dma_start(out=vector_rows[0:E, :], in_=b5[:, 0:P])
+        nc.scalar.dma_start(out=vector_rows[E : 2 * E, :], in_=b5[:, P : 2 * P])
+        nc.scalar.dma_start(out=vector_rows[2 * E : 2 * E + 1, :], in_=max_logvar)
+        nc.scalar.dma_start(out=vector_rows[2 * E + 1 : 2 * E + 2, :], in_=min_logvar)
         load_h3(0, 0, PAIR)
         w4_loaded[0] = load_words(W4_words, 0, H, "w4_loaded")
         load_scales(w4_scales_raw, W4_scales, 0)
-        nc.sync.dma_start(out=b4_rows[0:E, :], in_=b4)
-        nc.sync.dma_start(out=vector_rows[0:E, :], in_=b5[:, 0:P])
-        nc.sync.dma_start(out=vector_rows[E : 2 * E, :], in_=b5[:, P : 2 * P])
-        nc.sync.dma_start(out=vector_rows[2 * E : 2 * E + 1, :], in_=max_logvar)
-        nc.sync.dma_start(out=vector_rows[2 * E + 1 : 2 * E + 2, :], in_=min_logvar)
         load_h3(0, 1)
         load_scales(w5_scales, W5_scales, 0)
         w5_words[0] = load_words(W5_words, 0, 2 * P, "w5")
@@ -167,6 +170,7 @@ def tile_ensembledynamicsmodel_pa_e_kernel(
             nc.vector.tensor_copy(out=b4_cols[:], in_=b4_ps[:, :, 0:E])
             nc.vector.tensor_copy(out=vector_cols[:], in_=cols_ps[:, 0 : 2 * E + 2])
             nc.scalar.activation(out=exps[:], in_=vector_cols[:, 2 * E : 2 * E + 2], func=ACT.Exp)
+            nc.scalar.activation(out=warm[:], in_=exps[:, 0:1], func=ACT.Silu)
             nc.vector.tensor_scalar_mul(out=half_emax[:], in0=exps[:, 0:1], scalar1=0.5)
             nc.vector.tensor_add(out=var_mid[:], in0=exps[:, 1:2], in1=half_emax[:])
             nc.vector.tensor_scalar(
@@ -313,12 +317,14 @@ def tile_ensembledynamicsmodel_pa_e_kernel(
                 function(s, *args)
 
         def first_part_round(r):
-            stage(layer4, r, 0)
-            stage(layer4, r, 1)
+            if r > 0:
+                stage(layer4, r, 0)
+                stage(layer4, r, 1)
             stage(transpose_noise, r - 2)
             stage(transpose_h3, r + 2, 0)
-            stage(layer4, r, 2)
-            stage(layer4, r, 3)
+            if r > 0:
+                stage(layer4, r, 2)
+                stage(layer4, r, 3)
             stage(logvar, r - 2)
             stage(transpose_h3, r + 2, 1)
             stage(quantise_h3, r + 1)
@@ -337,11 +343,20 @@ def tile_ensembledynamicsmodel_pa_e_kernel(
                 if e % GROUP == 0:
                     reorder_w4_scales(e // GROUP)
 
-        first_part_round(-2)
-        column_constants()
-        reorder_w4_scales(0)
+        for pair in range(HALVES):
+            transpose_h3(0, pair)
+        copy_h3(nc.vector.tensor_copy, 0, 0)
+        copy_h3(nc.scalar.copy, 0, 1)
         reorder_w4(0)
-        for r in range(-1, STEPS + 2):
+        reorder_w4_scales(0)
+        quantise_h3(0)
+        column_constants()
+        for t in range(PACK):
+            layer4(0, t)
+        for pair in range(HALVES):
+            transpose_h3(1, pair)
+            copy_h3(nc.vector.tensor_copy, 1, pair)
+        for r in range(STEPS + 2):
             first_part_round(r)
 
         def half_columns(half):

@@ -21,10 +21,12 @@ PACK = 4
 TILES = B // P
 PAIR = 2
 QUAD = 4
+PAIRS = QUAD // PAIR
 HALVES = TILES // QUAD
 STEPS = E * HALVES
 N = QUAD * P
 LIVE_ROWS = 4
+DIRECT = (0, E - 1)
 GROUP = 4
 
 FLOPS = 2 * E * B * H * (H + 2 * P)
@@ -64,7 +66,6 @@ def tile_ensembledynamicsmodel_pa_e_kernel(
         w5_scales = keep.tile([P, groups, 2 * P], U8, align_bytes=64)
         warm = keep.tile([P, 1], F32)
         nc.vector.memset(warm[:], 0.0)
-        nc.scalar.activation(out=warm[:], in_=warm[:], func=ACT.Exp)
         b4_rows = keep.tile([P, H], BF16)
         nc.vector.memset(b4_rows[:], 0.0)
         vector_rows = keep.tile([P, P], BF16)
@@ -121,7 +122,8 @@ def tile_ensembledynamicsmodel_pa_e_kernel(
         nc.scalar.dma_start(out=vector_rows[E : 2 * E, :], in_=b5[:, P : 2 * P])
         nc.scalar.dma_start(out=vector_rows[2 * E : 2 * E + 1, :], in_=max_logvar)
         nc.scalar.dma_start(out=vector_rows[2 * E + 1 : 2 * E + 2, :], in_=min_logvar)
-        load_h3(0, 0, PAIR)
+        nc.scalar.activation(out=warm[:], in_=warm[:], func=ACT.Exp)
+        load_h3(0, 0, PAIRS)
         w4_loaded[0] = load_words(W4_words, 0, H, "w4_loaded")
         load_scales(w4_scales_raw, W4_scales, 0)
         load_h3(0, 1)
@@ -295,23 +297,6 @@ def tile_ensembledynamicsmodel_pa_e_kernel(
                 scale=0.5,
             )
 
-        def transpose_noise(s):
-            e, half = divmod(s, HALVES)
-            noise_ps = psum.tile([P, QUAD, P], BF16, tag="tn")
-            for i in range(QUAD):
-                nc.tensor.matmul(
-                    out=noise_ps[:, i, :],
-                    lhsT=noise_sb[e][:, half * QUAD + i, :],
-                    rhs=ident_bf16[:],
-                    start=True,
-                    stop=True,
-                )
-            live["noise_ps", s] = noise_ps
-
-        def copy_noise(s):
-            e, cols = member_of(s), columns_of(s)
-            nc.vector.tensor_copy(out=noise_t[e][:, cols], in_=live["noise_ps", s][:].rearrange("p i b -> p (i b)"))
-
         def stage(function, s, *args):
             if 0 <= s < STEPS:
                 function(s, *args)
@@ -320,7 +305,6 @@ def tile_ensembledynamicsmodel_pa_e_kernel(
             if r > 0:
                 stage(layer4, r, 0)
                 stage(layer4, r, 1)
-            stage(transpose_noise, r - 2)
             stage(transpose_h3, r + 2, 0)
             if r > 0:
                 stage(layer4, r, 2)
@@ -332,10 +316,10 @@ def tile_ensembledynamicsmodel_pa_e_kernel(
                 copy_h3(nc.vector.tensor_copy, r + 2, 0)
             stage(swish, r)
             stage(interleave_h4, r - 1)
-            stage(clamp_tanh, r - 2)
-            stage(copy_noise, r - 2)
+            if r - 2 < STEPS - 1:
+                stage(clamp_tanh, r - 2)
             if 0 <= r + 2 < STEPS:
-                copy_h3(nc.scalar.copy, r + 2, 1)
+                copy_h3(nc.vector.tensor_copy if r % 4 == 3 else nc.scalar.copy, r + 2, 1)
             stage(quantise_h4, r - 1)
             e, half = divmod(r + 2, HALVES)
             if half == 0 and 0 < e < E:
@@ -343,7 +327,7 @@ def tile_ensembledynamicsmodel_pa_e_kernel(
                 if e % GROUP == 0:
                     reorder_w4_scales(e // GROUP)
 
-        for pair in range(HALVES):
+        for pair in range(PAIRS):
             transpose_h3(0, pair)
         copy_h3(nc.vector.tensor_copy, 0, 0)
         copy_h3(nc.scalar.copy, 0, 1)
@@ -353,7 +337,7 @@ def tile_ensembledynamicsmodel_pa_e_kernel(
         column_constants()
         for t in range(PACK):
             layer4(0, t)
-        for pair in range(HALVES):
+        for pair in range(PAIRS):
             transpose_h3(1, pair)
             copy_h3(nc.vector.tensor_copy, 1, pair)
         for r in range(STEPS + 2):
@@ -362,21 +346,42 @@ def tile_ensembledynamicsmodel_pa_e_kernel(
         def half_columns(half):
             return slice(half * N, (half + 1) * N)
 
+        def transpose_noise(e):
+            noise_ps = psum.tile([P, TILES, P], BF16, tag=("tn", "a2")[e % 2], name="noise_ps")
+            for i in range(TILES):
+                nc.tensor.matmul(
+                    out=noise_ps[:, i, :], lhsT=noise_sb[e][:, i, :], rhs=ident_bf16[:], start=True, stop=True
+                )
+            live["noise_ps", e] = noise_ps
+
+        def copy_noise(copy, e):
+            copy(out=noise_t[e][:], in_=live["noise_ps", e][:].rearrange("p i b -> p (i b)"))
+
         def stds(e):
-            nc.scalar.activation(
-                out=clamped[e][:], in_=clamped[e][:], func=ACT.Sqrt, bias=var_mid[:], scale=half_emax[:]
-            )
+            for half in range(HALVES):
+                cols = half_columns(half)
+                nc.scalar.activation(
+                    out=clamped[e][:, cols], in_=clamped[e][:, cols], func=ACT.Sqrt, bias=var_mid[:], scale=half_emax[:]
+                )
 
         def spread_noise(e):
             for half in range(HALVES):
                 cols = half_columns(half)
-                nc.gpsimd.tensor_tensor(
-                    out=clamped[e][:, cols], in0=clamped[e][:, cols], in1=noise_t[e][:, cols], op=ALU.mult
-                )
+                if e in DIRECT:
+                    nc.vector.tensor_tensor(
+                        out=clamped[e][:, cols],
+                        in0=live["noise_ps", e][:, half * QUAD : (half + 1) * QUAD, :].rearrange("p i b -> p (i b)"),
+                        in1=clamped[e][:, cols],
+                        op=ALU.mult,
+                    )
+                else:
+                    nc.gpsimd.tensor_tensor(
+                        out=clamped[e][:, cols], in0=clamped[e][:, cols], in1=noise_t[e][:, cols], op=ALU.mult
+                    )
 
         def mean(e):
             for half in range(HALVES):
-                mean_ps = psum.tile([P, N], F32, tag="a%d" % (e % 2 * HALVES + half), name="mean_ps")
+                mean_ps = psum.tile([P, N], F32, tag="a%d" % half, name="mean_ps")
                 w5_pass(mean_ps[:], e, 0, half_columns(half))
                 live["mean", e, half] = mean_ps
 
@@ -419,13 +424,24 @@ def tile_ensembledynamicsmodel_pa_e_kernel(
             if 0 <= e < E:
                 function(e)
 
-        for r in range(-2, E):
+        transpose_noise(0)
+        transpose_noise(1)
+        copy_noise(nc.vector.tensor_copy, 1)
+        stds(0)
+        stds(1)
+        for r in range(-1, E):
             member_stage(mean, r + 1)
+            member_stage(spread_noise, r + 1)
+            member_stage(transpose_noise, r + 3)
             member_stage(transpose_back, r)
             member_stage(sample, r + 1)
             member_stage(finish, r)
-            member_stage(stds, r + 2)
-            member_stage(spread_noise, r + 2)
+            if r + 3 < E:
+                if r + 3 not in DIRECT:
+                    copy_noise(nc.scalar.copy, r + 3)
+                if r + 3 == E - 1:
+                    clamp_tanh(STEPS - 1)
+                stds(r + 3)
 
         nc.sync.dma_start(
             out=out_1.rearrange("e (p i) o -> p e (i o)", i=TILES),

@@ -66,6 +66,8 @@ def tile_ensembledynamicsmodel_pa_e_kernel(
         w5_scales = keep.tile([P, groups, 2 * P], U8, align_bytes=64)
         warm = keep.tile([P, 1], F32)
         nc.vector.memset(warm[:], 0.0)
+        zeros = keep.tile([P, N], BF16)
+        nc.vector.memset(zeros[:], 0.0)
         b4_rows = keep.tile([P, H], BF16)
         nc.vector.memset(b4_rows[:], 0.0)
         vector_rows = keep.tile([P, P], BF16)
@@ -117,16 +119,16 @@ def tile_ensembledynamicsmodel_pa_e_kernel(
             )
             noise_sb[e] = rows
 
-        nc.scalar.dma_start(out=b4_rows[0:E, :], in_=b4)
-        nc.scalar.dma_start(out=vector_rows[0:E, :], in_=b5[:, 0:P])
-        nc.scalar.dma_start(out=vector_rows[E : 2 * E, :], in_=b5[:, P : 2 * P])
-        nc.scalar.dma_start(out=vector_rows[2 * E : 2 * E + 1, :], in_=max_logvar)
-        nc.scalar.dma_start(out=vector_rows[2 * E + 1 : 2 * E + 2, :], in_=min_logvar)
+        nc.gpsimd.dma_start(out=b4_rows[0:E, :], in_=b4)
+        nc.gpsimd.dma_start(out=vector_rows[0:E, :], in_=b5[:, 0:P])
+        nc.gpsimd.dma_start(out=vector_rows[E : 2 * E, :], in_=b5[:, P : 2 * P])
+        nc.gpsimd.dma_start(out=vector_rows[2 * E : 2 * E + 1, :], in_=max_logvar)
+        nc.gpsimd.dma_start(out=vector_rows[2 * E + 1 : 2 * E + 2, :], in_=min_logvar)
         nc.scalar.activation(out=warm[:], in_=warm[:], func=ACT.Exp)
         load_h3(0, 0, PAIRS)
         w4_loaded[0] = load_words(W4_words, 0, H, "w4_loaded")
         load_scales(w4_scales_raw, W4_scales, 0)
-        load_h3(0, 1)
+        load_h3(0, 1, PAIRS)
         load_scales(w5_scales, W5_scales, 0)
         w5_words[0] = load_words(W5_words, 0, 2 * P, "w5")
         load_noise(0)
@@ -252,6 +254,8 @@ def tile_ensembledynamicsmodel_pa_e_kernel(
             e = member_of(s)
             h4 = work.tile([P, PACK, N], BF16, tag="h4")
             for t in range(PACK):
+                if t == PACK // 2:
+                    stage(clamp_tanh, s - 2)
                 nc.scalar.activation(
                     out=h4[:, t, :], in_=live["acc", s, t][:], func=ACT.Silu, bias=b4_cols[:, t, e : e + 1]
                 )
@@ -259,7 +263,10 @@ def tile_ensembledynamicsmodel_pa_e_kernel(
 
         def interleave_h4(s):
             grouped = work.tile([P, N, PACK], BF16, tag="h4_grouped", align_bytes=64)
-            nc.vector.tensor_copy(out=grouped[:], in_=live["h4", s][:].rearrange("p t b -> p b t"))
+            nc.vector.tensor_copy(
+                out=grouped[:].rearrange("p (c i) t -> p c t i", i=PACK),
+                in_=live["h4", s][:].rearrange("p t (c i) -> p c t i", i=PACK),
+            )
             live["h4_grouped", s] = grouped
 
         def quantise_h4(s):
@@ -282,8 +289,8 @@ def tile_ensembledynamicsmodel_pa_e_kernel(
                 stop=True,
             )
 
-        def logvar(s):
-            lv = psum.tile([P, N], F32, tag="tl")
+        def logvar(s, bank="tl"):
+            lv = psum.tile([P, N], F32, tag=bank, name="lv")
             w5_pass(lv[:], member_of(s), P, columns_of(s))
             live["lv", s] = lv
 
@@ -316,8 +323,6 @@ def tile_ensembledynamicsmodel_pa_e_kernel(
                 copy_h3(nc.vector.tensor_copy, r + 2, 0)
             stage(swish, r)
             stage(interleave_h4, r - 1)
-            if r - 2 < STEPS - 1:
-                stage(clamp_tanh, r - 2)
             if 0 <= r + 2 < STEPS:
                 copy_h3(nc.vector.tensor_copy if r % 4 == 3 else nc.scalar.copy, r + 2, 1)
             stage(quantise_h4, r - 1)
@@ -327,6 +332,12 @@ def tile_ensembledynamicsmodel_pa_e_kernel(
                 if e % GROUP == 0:
                     reorder_w4_scales(e // GROUP)
 
+        def warm_up(passes):
+            for i in range(passes):
+                scratch = psum.tile([P, N], F32, tag="tl", name="scratch")
+                nc.tensor.matmul(out=scratch[:], lhsT=zeros[:, 0:P], rhs=zeros[:], start=True, stop=True)
+
+        warm_up(5)
         for pair in range(PAIRS):
             transpose_h3(0, pair)
         copy_h3(nc.vector.tensor_copy, 0, 0)
@@ -334,20 +345,22 @@ def tile_ensembledynamicsmodel_pa_e_kernel(
         reorder_w4(0)
         reorder_w4_scales(0)
         quantise_h3(0)
+        warm_up(3)
+        transpose_h3(1, 0)
         column_constants()
+        copy_h3(nc.vector.tensor_copy, 1, 0)
         for t in range(PACK):
             layer4(0, t)
-        for pair in range(PAIRS):
-            transpose_h3(1, pair)
-            copy_h3(nc.vector.tensor_copy, 1, pair)
-        for r in range(STEPS + 2):
+        transpose_h3(1, 1)
+        copy_h3(nc.vector.tensor_copy, 1, 1)
+        for r in range(STEPS):
             first_part_round(r)
 
         def half_columns(half):
             return slice(half * N, (half + 1) * N)
 
         def transpose_noise(e):
-            noise_ps = psum.tile([P, TILES, P], BF16, tag=("tn", "a2")[e % 2], name="noise_ps")
+            noise_ps = psum.tile([P, TILES, P], BF16, tag=("tn", "tl")[e % 2], name="noise_ps")
             for i in range(TILES):
                 nc.tensor.matmul(
                     out=noise_ps[:, i, :], lhsT=noise_sb[e][:, i, :], rhs=ident_bf16[:], start=True, stop=True
@@ -426,6 +439,8 @@ def tile_ensembledynamicsmodel_pa_e_kernel(
 
         transpose_noise(0)
         transpose_noise(1)
+        interleave_h4(STEPS - 1)
+        quantise_h4(STEPS - 1)
         copy_noise(nc.vector.tensor_copy, 1)
         stds(0)
         stds(1)
@@ -439,9 +454,12 @@ def tile_ensembledynamicsmodel_pa_e_kernel(
             if r + 3 < E:
                 if r + 3 not in DIRECT:
                     copy_noise(nc.scalar.copy, r + 3)
-                if r + 3 == E - 1:
-                    clamp_tanh(STEPS - 1)
                 stds(r + 3)
+            if r == 0:
+                for half in range(HALVES):
+                    s = (E - 1) * HALVES + half
+                    logvar(s, ("a2", "a3")[half])
+                    clamp_tanh(s)
 
         nc.sync.dma_start(
             out=out_1.rearrange("e (p i) o -> p e (i o)", i=TILES),

@@ -119,15 +119,14 @@ def tile_ensembledynamicsmodel_pa_e_kernel(
             )
             noise_sb[e] = rows
 
-        nc.gpsimd.dma_start(out=b4_rows[0:E, :], in_=b4)
-        nc.gpsimd.dma_start(out=vector_rows[0:E, :], in_=b5[:, 0:P])
-        nc.gpsimd.dma_start(out=vector_rows[E : 2 * E, :], in_=b5[:, P : 2 * P])
-        nc.gpsimd.dma_start(out=vector_rows[2 * E : 2 * E + 1, :], in_=max_logvar)
-        nc.gpsimd.dma_start(out=vector_rows[2 * E + 1 : 2 * E + 2, :], in_=min_logvar)
         nc.scalar.activation(out=warm[:], in_=warm[:], func=ACT.Exp)
         load_h3(0, 0, PAIRS)
         w4_loaded[0] = load_words(W4_words, 0, H, "w4_loaded")
         load_scales(w4_scales_raw, W4_scales, 0)
+        nc.sync.dma_start(out=b4_rows[0:E, :], in_=b4)
+        nc.sync.dma_start(out=vector_rows[0 : 2 * E, :], in_=b5.rearrange("e (h c) -> h e c", h=2))
+        nc.sync.dma_start(out=vector_rows[2 * E : 2 * E + 1, :], in_=max_logvar)
+        nc.sync.dma_start(out=vector_rows[2 * E + 1 : 2 * E + 2, :], in_=min_logvar)
         load_h3(0, 1, PAIRS)
         load_scales(w5_scales, W5_scales, 0)
         w5_words[0] = load_words(W5_words, 0, 2 * P, "w5")
@@ -304,6 +303,17 @@ def tile_ensembledynamicsmodel_pa_e_kernel(
                 scale=0.5,
             )
 
+        def transpose_noise(e):
+            noise_ps = psum.tile([P, TILES, P], BF16, tag="tn")
+            for i in range(TILES):
+                nc.tensor.matmul(
+                    out=noise_ps[:, i, :], lhsT=noise_sb[e][:, i, :], rhs=ident_bf16[:], start=True, stop=True
+                )
+            live["noise_ps", e] = noise_ps
+
+        def copy_noise(copy, e):
+            copy(out=noise_t[e][:], in_=live["noise_ps", e][:].rearrange("p i b -> p (i b)"))
+
         def stage(function, s, *args):
             if 0 <= s < STEPS:
                 function(s, *args)
@@ -326,18 +336,22 @@ def tile_ensembledynamicsmodel_pa_e_kernel(
             if 0 <= r + 2 < STEPS:
                 copy_h3(nc.vector.tensor_copy if r % 4 == 3 else nc.scalar.copy, r + 2, 1)
             stage(quantise_h4, r - 1)
+            if r + 2 >= STEPS:
+                for e in ((1,), (2, 3))[r + 2 - STEPS]:
+                    transpose_noise(e)
+                    copy_noise(nc.vector.tensor_copy, e)
             e, half = divmod(r + 2, HALVES)
             if half == 0 and 0 < e < E:
                 reorder_w4(e)
                 if e % GROUP == 0:
                     reorder_w4_scales(e // GROUP)
 
-        def warm_up(passes):
-            for i in range(passes):
-                scratch = psum.tile([P, N], F32, tag="tl", name="scratch")
+        def warm_up():
+            for t in range(PACK - 1):
+                scratch = psum.tile([P, N], F32, tag="a%d" % t, name="scratch")
                 nc.tensor.matmul(out=scratch[:], lhsT=zeros[:, 0:P], rhs=zeros[:], start=True, stop=True)
 
-        warm_up(5)
+        warm_up()
         for pair in range(PAIRS):
             transpose_h3(0, pair)
         copy_h3(nc.vector.tensor_copy, 0, 0)
@@ -345,7 +359,7 @@ def tile_ensembledynamicsmodel_pa_e_kernel(
         reorder_w4(0)
         reorder_w4_scales(0)
         quantise_h3(0)
-        warm_up(3)
+        warm_up()
         transpose_h3(1, 0)
         column_constants()
         copy_h3(nc.vector.tensor_copy, 1, 0)
@@ -358,17 +372,6 @@ def tile_ensembledynamicsmodel_pa_e_kernel(
 
         def half_columns(half):
             return slice(half * N, (half + 1) * N)
-
-        def transpose_noise(e):
-            noise_ps = psum.tile([P, TILES, P], BF16, tag=("tn", "tl")[e % 2], name="noise_ps")
-            for i in range(TILES):
-                nc.tensor.matmul(
-                    out=noise_ps[:, i, :], lhsT=noise_sb[e][:, i, :], rhs=ident_bf16[:], start=True, stop=True
-                )
-            live["noise_ps", e] = noise_ps
-
-        def copy_noise(copy, e):
-            copy(out=noise_t[e][:], in_=live["noise_ps", e][:].rearrange("p i b -> p (i b)"))
 
         def stds(e):
             for half in range(HALVES):
@@ -438,28 +441,31 @@ def tile_ensembledynamicsmodel_pa_e_kernel(
                 function(e)
 
         transpose_noise(0)
-        transpose_noise(1)
         interleave_h4(STEPS - 1)
         quantise_h4(STEPS - 1)
-        copy_noise(nc.vector.tensor_copy, 1)
-        stds(0)
-        stds(1)
+        for e in range(4):
+            stds(e)
+        mean(0)
+        for half in range(HALVES):
+            logvar((E - 1) * HALVES + half, ("a2", "a3")[half])
         for r in range(-1, E):
-            member_stage(mean, r + 1)
+            if r >= 0:
+                member_stage(mean, r + 1)
             member_stage(spread_noise, r + 1)
-            member_stage(transpose_noise, r + 3)
             member_stage(transpose_back, r)
             member_stage(sample, r + 1)
             member_stage(finish, r)
-            if r + 3 < E:
-                if r + 3 not in DIRECT:
-                    copy_noise(nc.scalar.copy, r + 3)
-                stds(r + 3)
-            if r == 0:
+            if r == -1:
+                transpose_noise(4)
+                copy_noise(nc.scalar.copy, 4)
                 for half in range(HALVES):
-                    s = (E - 1) * HALVES + half
-                    logvar(s, ("a2", "a3")[half])
-                    clamp_tanh(s)
+                    clamp_tanh((E - 1) * HALVES + half)
+                stds(4)
+                transpose_noise(5)
+                copy_noise(nc.scalar.copy, 5)
+                stds(5)
+                transpose_noise(6)
+                stds(6)
 
         nc.sync.dma_start(
             out=out_1.rearrange("e (p i) o -> p e (i o)", i=TILES),

@@ -64,14 +64,16 @@ def tile_ensembledynamicsmodel_pa_e_kernel(
         w4_scales_raw = keep.tile([P, groups, H], U8, align_bytes=64)
         w4_scales = keep.tile([P, groups, PACK, P], U8, align_bytes=64)
         w5_scales = keep.tile([P, groups, 2 * P], U8, align_bytes=64)
+        limit_rows = keep.tile([P, P], BF16)
+        nc.vector.memset(limit_rows[:], 0.0)
         warm = keep.tile([P, 1], F32)
         nc.vector.memset(warm[:], 0.0)
         zeros = keep.tile([P, N], BF16)
         nc.vector.memset(zeros[:], 0.0)
         b4_rows = keep.tile([P, H], BF16)
         nc.vector.memset(b4_rows[:], 0.0)
-        vector_rows = keep.tile([P, P], BF16)
-        nc.vector.memset(vector_rows[:], 0.0)
+        b5_rows = keep.tile([P, P], BF16)
+        nc.vector.memset(b5_rows[:], 0.0)
         nc.vector.memset(w4_scales_raw[:].rearrange("p g n -> p (g n)").bitcast(I32), 0)
         nc.vector.memset(w5_scales[:].rearrange("p g n -> p (g n)").bitcast(I32), 0)
 
@@ -120,14 +122,14 @@ def tile_ensembledynamicsmodel_pa_e_kernel(
             noise_sb[e] = rows
 
         nc.scalar.activation(out=warm[:], in_=warm[:], func=ACT.Exp)
+        nc.sync.dma_start(out=limit_rows[0:1, :], in_=max_logvar)
+        nc.sync.dma_start(out=limit_rows[1:2, :], in_=min_logvar)
         load_h3(0, 0, PAIRS)
         w4_loaded[0] = load_words(W4_words, 0, H, "w4_loaded")
         load_scales(w4_scales_raw, W4_scales, 0)
+        load_h3(0, 1)
         nc.sync.dma_start(out=b4_rows[0:E, :], in_=b4)
-        nc.sync.dma_start(out=vector_rows[0 : 2 * E, :], in_=b5.rearrange("e (h c) -> h e c", h=2))
-        nc.sync.dma_start(out=vector_rows[2 * E : 2 * E + 1, :], in_=max_logvar)
-        nc.sync.dma_start(out=vector_rows[2 * E + 1 : 2 * E + 2, :], in_=min_logvar)
-        load_h3(0, 1, PAIRS)
+        nc.sync.dma_start(out=b5_rows[0 : 2 * E, :], in_=b5.rearrange("e (h c) -> h e c", h=2))
         load_scales(w5_scales, W5_scales, 0)
         w5_words[0] = load_words(W5_words, 0, 2 * P, "w5")
         load_noise(0)
@@ -158,32 +160,37 @@ def tile_ensembledynamicsmodel_pa_e_kernel(
         rewards_sb = keep.tile([P, E, TILES, 1], F32)
 
         b4_cols = keep.tile([P, PACK, E], F32)
-        vector_cols = keep.tile([P, 2 * E + 2], F32)
+        b5_cols = keep.tile([P, 2 * E], F32)
+        limit_cols = keep.tile([P, 2], F32)
         exps = keep.tile([P, 2], F32)
         half_emax = keep.tile([P, 1], F32)
         var_mid = keep.tile([P, 1], F32)
         tanh_bias = keep.tile([P, E], F32)
 
-        def column_constants():
+        def columns_of_limits():
+            limit_ps = psum.tile([P, P], BF16, tag="tl")
+            nc.tensor.transpose(limit_ps[:], limit_rows[:], ident_bf16[:])
+            nc.vector.tensor_copy(out=limit_cols[:], in_=limit_ps[:, 0:2])
+            nc.scalar.activation(out=exps[:], in_=limit_cols[:], func=ACT.Exp)
+
+        def columns_of_biases():
             b4_ps = psum.tile([P, PACK, P], BF16, tag="tn")
             for t in range(PACK):
                 nc.tensor.transpose(b4_ps[:, t, :], b4_rows[:, t::PACK], ident_bf16[:])
-            cols_ps = psum.tile([P, P], BF16, tag="tl")
-            nc.tensor.transpose(cols_ps[:], vector_rows[:], ident_bf16[:])
+            b5_ps = psum.tile([P, P], BF16, tag="tl")
+            nc.tensor.transpose(b5_ps[:], b5_rows[:], ident_bf16[:])
             nc.vector.tensor_copy(out=b4_cols[:], in_=b4_ps[:, :, 0:E])
-            nc.vector.tensor_copy(out=vector_cols[:], in_=cols_ps[:, 0 : 2 * E + 2])
-            nc.scalar.activation(out=exps[:], in_=vector_cols[:, 2 * E : 2 * E + 2], func=ACT.Exp)
-            nc.scalar.activation(out=warm[:], in_=exps[:, 0:1], func=ACT.Silu)
-            nc.vector.tensor_scalar_mul(out=half_emax[:], in0=exps[:, 0:1], scalar1=0.5)
-            nc.vector.tensor_add(out=var_mid[:], in0=exps[:, 1:2], in1=half_emax[:])
+            nc.vector.tensor_copy(out=b5_cols[:], in_=b5_ps[:, 0 : 2 * E])
             nc.vector.tensor_scalar(
                 out=tanh_bias[:],
-                in0=vector_cols[:, E : 2 * E],
-                scalar1=vector_cols[:, 2 * E : 2 * E + 1],
+                in0=b5_cols[:, E : 2 * E],
+                scalar1=limit_cols[:, 0:1],
                 scalar2=0.5,
                 op0=ALU.subtract,
                 op1=ALU.mult,
             )
+            nc.vector.tensor_scalar_mul(out=half_emax[:], in0=exps[:, 0:1], scalar1=0.5)
+            nc.vector.tensor_add(out=var_mid[:], in0=exps[:, 1:2], in1=half_emax[:])
 
         def reorder_w4_scales(group):
             nc.vector.tensor_copy(
@@ -304,7 +311,7 @@ def tile_ensembledynamicsmodel_pa_e_kernel(
             )
 
         def transpose_noise(e):
-            noise_ps = psum.tile([P, TILES, P], BF16, tag="tn")
+            noise_ps = psum.tile([P, TILES, P], BF16, tag=("tn", "tl")[e in (3, 5)], name="noise_ps")
             for i in range(TILES):
                 nc.tensor.matmul(
                     out=noise_ps[:, i, :], lhsT=noise_sb[e][:, i, :], rhs=ident_bf16[:], start=True, stop=True
@@ -337,9 +344,8 @@ def tile_ensembledynamicsmodel_pa_e_kernel(
                 copy_h3(nc.vector.tensor_copy if r % 4 == 3 else nc.scalar.copy, r + 2, 1)
             stage(quantise_h4, r - 1)
             if r + 2 >= STEPS:
-                for e in ((1,), (2, 3))[r + 2 - STEPS]:
-                    transpose_noise(e)
-                    copy_noise(nc.vector.tensor_copy, e)
+                transpose_noise(r + 3 - STEPS)
+                copy_noise(nc.vector.tensor_copy, r + 3 - STEPS)
             e, half = divmod(r + 2, HALVES)
             if half == 0 and 0 < e < E:
                 reorder_w4(e)
@@ -352,19 +358,22 @@ def tile_ensembledynamicsmodel_pa_e_kernel(
                 nc.tensor.matmul(out=scratch[:], lhsT=zeros[:, 0:P], rhs=zeros[:], start=True, stop=True)
 
         warm_up()
+        columns_of_limits()
         for pair in range(PAIRS):
             transpose_h3(0, pair)
         copy_h3(nc.vector.tensor_copy, 0, 0)
         copy_h3(nc.scalar.copy, 0, 1)
+        nc.scalar.activation(out=warm[:], in_=exps[:, 0:1], func=ACT.Silu)
         reorder_w4(0)
         reorder_w4_scales(0)
         quantise_h3(0)
-        warm_up()
+        columns_of_biases()
+        layer4(0, 0)
+        layer4(0, 1)
         transpose_h3(1, 0)
-        column_constants()
         copy_h3(nc.vector.tensor_copy, 1, 0)
-        for t in range(PACK):
-            layer4(0, t)
+        layer4(0, 2)
+        layer4(0, 3)
         transpose_h3(1, 1)
         copy_h3(nc.vector.tensor_copy, 1, 1)
         for r in range(STEPS):
@@ -407,7 +416,7 @@ def tile_ensembledynamicsmodel_pa_e_kernel(
                 nc.vector.scalar_tensor_tensor(
                     out=samples[:],
                     in0=live["mean", e, half][:],
-                    scalar=vector_cols[:, e : e + 1],
+                    scalar=b5_cols[:, e : e + 1],
                     in1=clamped[e][:, half_columns(half)],
                     op0=ALU.add,
                     op1=ALU.add,
@@ -443,7 +452,7 @@ def tile_ensembledynamicsmodel_pa_e_kernel(
         transpose_noise(0)
         interleave_h4(STEPS - 1)
         quantise_h4(STEPS - 1)
-        for e in range(4):
+        for e in range(3):
             stds(e)
         mean(0)
         for half in range(HALVES):
@@ -453,19 +462,16 @@ def tile_ensembledynamicsmodel_pa_e_kernel(
                 member_stage(mean, r + 1)
             member_stage(spread_noise, r + 1)
             member_stage(transpose_back, r)
+            member_stage(transpose_noise, r + 4)
             member_stage(sample, r + 1)
             member_stage(finish, r)
-            if r == -1:
-                transpose_noise(4)
-                copy_noise(nc.scalar.copy, 4)
-                for half in range(HALVES):
-                    clamp_tanh((E - 1) * HALVES + half)
-                stds(4)
-                transpose_noise(5)
-                copy_noise(nc.scalar.copy, 5)
-                stds(5)
-                transpose_noise(6)
-                stds(6)
+            if r + 4 < E:
+                if r + 4 not in DIRECT:
+                    copy_noise(nc.scalar.copy, r + 4)
+                if r == 0:
+                    for half in range(HALVES):
+                        clamp_tanh((E - 1) * HALVES + half)
+                stds(r + 4)
 
         nc.sync.dma_start(
             out=out_1.rearrange("e (p i) o -> p e (i o)", i=TILES),

@@ -26,7 +26,7 @@ HALVES = TILES // QUAD
 STEPS = E * HALVES
 N = QUAD * P
 LIVE_ROWS = 4
-DIRECT = (0, E - 1)
+DIRECT = (0,)
 GROUP = 4
 
 FLOPS = 2 * E * B * H * (H + 2 * P)
@@ -130,17 +130,17 @@ def tile_ensembledynamicsmodel_pa_e_kernel(
         load_h3(0, 1)
         nc.sync.dma_start(out=b4_rows[0:E, :], in_=b4)
         nc.sync.dma_start(out=b5_rows[0 : 2 * E, :], in_=b5.rearrange("e (h c) -> h e c", h=2))
-        load_scales(w5_scales, W5_scales, 0)
-        w5_words[0] = load_words(W5_words, 0, 2 * P, "w5")
-        load_noise(0)
-        for e in range(1, E):
-            load_h3(e, 0)
-            w4_loaded[e] = load_words(W4_words, e, H, "w4_loaded")
-            if e % GROUP == 0:
-                load_scales(w4_scales_raw, W4_scales, e // GROUP)
-                load_scales(w5_scales, W5_scales, e // GROUP)
-            load_h3(e, 1)
-            w5_words[e] = load_words(W5_words, e, 2 * P, "w5")
+        for e in range(1, E + 1):
+            if e < E:
+                load_h3(e, 0)
+                w4_loaded[e] = load_words(W4_words, e, H, "w4_loaded")
+                if e % GROUP == 0:
+                    load_scales(w4_scales_raw, W4_scales, e // GROUP)
+                load_h3(e, 1)
+            if (e - 1) % GROUP == 0:
+                load_scales(w5_scales, W5_scales, (e - 1) // GROUP)
+            w5_words[e - 1] = load_words(W5_words, e - 1, 2 * P, "w5")
+        for e in range(E):
             load_noise(e)
         state_sb = keep.tile([P, TILES, S], BF16)
         nc.sync.dma_start(
@@ -156,7 +156,8 @@ def tile_ensembledynamicsmodel_pa_e_kernel(
             h4_codes[e] = keep.tile([P, B], U32, name="h4_codes_%d" % e, align_bytes=64)
             h4_scales[e] = keep.tile([P, B], U8, name="h4_scales_%d" % e, align_bytes=64)
             clamped[e] = keep.tile([P, B], F32, name="clamped_%d" % e)
-            noise_t[e] = keep.tile([P, B], BF16, name="noise_t_%d" % e)
+            if e not in DIRECT:
+                noise_t[e] = keep.tile([P, B], BF16, name="noise_t_%d" % e)
         rewards_sb = keep.tile([P, E, TILES, 1], F32)
 
         b4_cols = keep.tile([P, PACK, E], F32)
@@ -336,12 +337,12 @@ def tile_ensembledynamicsmodel_pa_e_kernel(
             stage(logvar, r - 2)
             stage(transpose_h3, r + 2, 1)
             stage(quantise_h3, r + 1)
-            if 0 <= r + 2 < STEPS:
-                copy_h3(nc.vector.tensor_copy, r + 2, 0)
             stage(swish, r)
             stage(interleave_h4, r - 1)
             if 0 <= r + 2 < STEPS:
-                copy_h3(nc.vector.tensor_copy if r % 4 == 3 else nc.scalar.copy, r + 2, 1)
+                copy_h3(nc.vector.tensor_copy, r + 2, 0)
+            if 0 <= r + 2 < STEPS:
+                copy_h3(nc.scalar.copy, r + 2, 1)
             stage(quantise_h4, r - 1)
             if r + 2 >= STEPS:
                 transpose_noise(r + 3 - STEPS)
@@ -432,7 +433,7 @@ def tile_ensembledynamicsmodel_pa_e_kernel(
                 live["back", e, half] = back
 
         def finish(e):
-            next_states = work.tile([P, TILES, S], F32, tag="next_states")
+            next_states = work.tile([P, TILES, S], F32, tag="next_states", bufs=3)
             for half in range(HALVES):
                 tiles = slice(half * QUAD, (half + 1) * QUAD)
                 back = live["back", e, half]
@@ -466,9 +467,8 @@ def tile_ensembledynamicsmodel_pa_e_kernel(
             member_stage(sample, r + 1)
             member_stage(finish, r)
             if r + 4 < E:
-                if r + 4 not in DIRECT:
-                    copy_noise(nc.scalar.copy, r + 4)
-                if r == 0:
+                copy_noise(nc.scalar.copy, r + 4)
+                if r + 4 == E - 1:
                     for half in range(HALVES):
                         clamp_tanh((E - 1) * HALVES + half)
                 stds(r + 4)

@@ -342,7 +342,7 @@ def tile_ensembledynamicsmodel_pa_e_kernel(
             if 0 <= r + 2 < STEPS:
                 copy_h3(nc.vector.tensor_copy, r + 2, 0)
             if 0 <= r + 2 < STEPS:
-                copy_h3(nc.scalar.copy, r + 2, 1)
+                copy_h3(nc.scalar.copy if r % 2 == 0 else nc.vector.tensor_copy, r + 2, 1)
             stage(quantise_h4, r - 1)
             if r + 2 >= STEPS:
                 transpose_noise(r + 3 - STEPS)
@@ -432,6 +432,12 @@ def tile_ensembledynamicsmodel_pa_e_kernel(
                     nc.tensor.transpose(back[:, j, :], samples[:, j * P : (j + 1) * P], ident_f32[:])
                 live["back", e, half] = back
 
+        def store_rewards(first, last):
+            nc.sync.dma_start(
+                out=out_1[first:last].rearrange("e (p i) o -> p e (i o)", i=TILES),
+                in_=rewards_sb[:, first:last].rearrange("p e i o -> p e (i o)"),
+            )
+
         def finish(e):
             next_states = work.tile([P, TILES, S], F32, tag="next_states", bufs=3)
             for half in range(HALVES):
@@ -445,6 +451,8 @@ def tile_ensembledynamicsmodel_pa_e_kernel(
                 out=out_0[e].rearrange("(p i) s -> p (i s)", i=TILES),
                 in_=next_states[:].rearrange("p i s -> p (i s)"),
             )
+            if e == E - 2:
+                store_rewards(0, E - 1)
 
         def member_stage(function, e):
             if 0 <= e < E:
@@ -473,7 +481,4 @@ def tile_ensembledynamicsmodel_pa_e_kernel(
                         clamp_tanh((E - 1) * HALVES + half)
                 stds(r + 4)
 
-        nc.sync.dma_start(
-            out=out_1.rearrange("e (p i) o -> p e (i o)", i=TILES),
-            in_=rewards_sb[:].rearrange("p e i o -> p e (i o)"),
-        )
+        store_rewards(E - 1, E)

@@ -26,7 +26,9 @@ HALVES = TILES // QUAD
 STEPS = E * HALVES
 N = QUAD * P
 LIVE_ROWS = 4
-DIRECT = (0,)
+DIRECT = (0, 5, 6)
+LATE = 5
+X_BANKS = 3
 GROUP = 4
 
 FLOPS = 2 * E * B * H * (H + 2 * P)
@@ -175,7 +177,7 @@ def tile_ensembledynamicsmodel_pa_e_kernel(
             nc.scalar.activation(out=exps[:], in_=limit_cols[:], func=ACT.Exp)
 
         def columns_of_biases():
-            b4_ps = psum.tile([P, PACK, P], BF16, tag="tn")
+            b4_ps = psum.tile([P, PACK, P], BF16, tag="a3", name="b4_ps")
             for t in range(PACK):
                 nc.tensor.transpose(b4_ps[:, t, :], b4_rows[:, t::PACK], ident_bf16[:])
             b5_ps = psum.tile([P, P], BF16, tag="tl")
@@ -217,7 +219,7 @@ def tile_ensembledynamicsmodel_pa_e_kernel(
 
         def transpose_h3(s, pair):
             words = h3_sb[divmod(s, HALVES)][:].bitcast(F32)
-            xt = psum.tile([P, PAIR, 2, P], F32, tag="tx", bufs=2)
+            xt = psum.tile([P, PAIR, 2, P], F32, tag="x%d" % ((s * PAIRS + pair) % X_BANKS), name="xt")
             for i in range(PAIR):
                 first = (pair * PAIR + i) * (H // 2)
                 for u in range(2):
@@ -262,7 +264,8 @@ def tile_ensembledynamicsmodel_pa_e_kernel(
             h4 = work.tile([P, PACK, N], BF16, tag="h4")
             for t in range(PACK):
                 if t == PACK // 2:
-                    stage(clamp_tanh, s - 2)
+                    if member_of(s - 2) < LATE:
+                        stage(clamp_tanh, s - 2)
                 nc.scalar.activation(
                     out=h4[:, t, :], in_=live["acc", s, t][:], func=ACT.Silu, bias=b4_cols[:, t, e : e + 1]
                 )
@@ -312,7 +315,7 @@ def tile_ensembledynamicsmodel_pa_e_kernel(
             )
 
         def transpose_noise(e):
-            noise_ps = psum.tile([P, TILES, P], BF16, tag=("tn", "tl")[e in (3, 5)], name="noise_ps")
+            noise_ps = psum.tile([P, TILES, P], BF16, tag=("x2", "tl")[e in (2, 4, 6)], name="noise_ps")
             for i in range(TILES):
                 nc.tensor.matmul(
                     out=noise_ps[:, i, :], lhsT=noise_sb[e][:, i, :], rhs=ident_bf16[:], start=True, stop=True
@@ -334,7 +337,8 @@ def tile_ensembledynamicsmodel_pa_e_kernel(
             if r > 0:
                 stage(layer4, r, 2)
                 stage(layer4, r, 3)
-            stage(logvar, r - 2)
+            if member_of(r - 2) < LATE:
+                stage(logvar, r - 2)
             stage(transpose_h3, r + 2, 1)
             stage(quantise_h3, r + 1)
             stage(swish, r)
@@ -342,11 +346,11 @@ def tile_ensembledynamicsmodel_pa_e_kernel(
             if 0 <= r + 2 < STEPS:
                 copy_h3(nc.vector.tensor_copy, r + 2, 0)
             if 0 <= r + 2 < STEPS:
-                copy_h3(nc.scalar.copy if r % 2 == 0 else nc.vector.tensor_copy, r + 2, 1)
+                copy_h3(nc.scalar.copy, r + 2, 1)
             stage(quantise_h4, r - 1)
-            if r + 2 >= STEPS:
-                transpose_noise(r + 3 - STEPS)
-                copy_noise(nc.vector.tensor_copy, r + 3 - STEPS)
+            if r + 2 == STEPS:
+                transpose_noise(1)
+                copy_noise(nc.vector.tensor_copy, 1)
             e, half = divmod(r + 2, HALVES)
             if half == 0 and 0 < e < E:
                 reorder_w4(e)
@@ -427,7 +431,7 @@ def tile_ensembledynamicsmodel_pa_e_kernel(
         def transpose_back(e):
             for half in range(HALVES):
                 samples = live["samples", e, half]
-                back = psum.tile([P, QUAD, P], F32, tag="tx", bufs=2)
+                back = psum.tile([P, QUAD, P], F32, tag="x%d" % half, name="back")
                 for j in range(QUAD):
                     nc.tensor.transpose(back[:, j, :], samples[:, j * P : (j + 1) * P], ident_f32[:])
                 live["back", e, half] = back
@@ -459,26 +463,41 @@ def tile_ensembledynamicsmodel_pa_e_kernel(
                 function(e)
 
         transpose_noise(0)
+        transpose_noise(2)
         interleave_h4(STEPS - 1)
         quantise_h4(STEPS - 1)
         for e in range(3):
             stds(e)
+        def late_logvars(e):
+            for half in range(HALVES):
+                logvar(e * HALVES + half, ("a2", "a3")[half])
+
+        def late_tanhs(e):
+            for half in range(HALVES):
+                clamp_tanh(e * HALVES + half)
+
         mean(0)
-        for half in range(HALVES):
-            logvar((E - 1) * HALVES + half, ("a2", "a3")[half])
+        late_logvars(LATE)
         for r in range(-1, E):
             if r >= 0:
                 member_stage(mean, r + 1)
             member_stage(spread_noise, r + 1)
             member_stage(transpose_back, r)
             member_stage(transpose_noise, r + 4)
-            member_stage(sample, r + 1)
-            member_stage(finish, r)
-            if r + 4 < E:
-                copy_noise(nc.scalar.copy, r + 4)
-                if r + 4 == E - 1:
-                    for half in range(HALVES):
-                        clamp_tanh((E - 1) * HALVES + half)
+            if r + 4 < LATE:
                 stds(r + 4)
+            if r + 4 < E and r + 4 not in DIRECT:
+                copy_noise(nc.scalar.copy, r + 4)
+            if r + 4 == LATE:
+                late_tanhs(LATE)
+            if r + 4 == LATE + 1:
+                late_logvars(LATE + 1)
+                late_tanhs(LATE + 1)
+                stds(LATE)
+                stds(LATE + 1)
+            member_stage(sample, r + 1)
+            if r == -1:
+                copy_noise(nc.vector.tensor_copy, 2)
+            member_stage(finish, r)
 
         store_rewards(E - 1, E)

@@ -263,7 +263,7 @@ def tile_ensembledynamicsmodel_pa_e_kernel(
             e = member_of(s)
             h4 = work.tile([P, PACK, N], BF16, tag="h4")
             for t in range(PACK):
-                if t == PACK // 2:
+                if t == PACK - 1:
                     if member_of(s - 2) < LATE:
                         stage(clamp_tanh, s - 2)
                 nc.scalar.activation(
@@ -376,7 +376,7 @@ def tile_ensembledynamicsmodel_pa_e_kernel(
         layer4(0, 0)
         layer4(0, 1)
         transpose_h3(1, 0)
-        copy_h3(nc.vector.tensor_copy, 1, 0)
+        copy_h3(nc.scalar.copy, 1, 0)
         layer4(0, 2)
         layer4(0, 3)
         transpose_h3(1, 1)

from contextlib import ExitStack

import concourse.mybir as mybir
from concourse.masks import make_identity

F32 = mybir.dt.float32
BF16 = mybir.dt.bfloat16
I32 = mybir.dt.int32
U32 = mybir.dt.uint32
U8 = mybir.dt.uint8
FP8X4 = mybir.dt.float8_e4m3fn_x4
ACT = mybir.ActivationFunctionType
ALU = mybir.AluOpType

E = 7
B = 1024
H = 512
S = 127
P = 128
PACK = 4
TILES = B // P
PAIR = 2
QUAD = 4
PAIRS = QUAD // PAIR
HALVES = TILES // QUAD
STEPS = E * HALVES
N = QUAD * P
LIVE_ROWS = 4
DIRECT = (0, 5, 6)
LATE = 5
X_BANKS = 3
GROUP = 4

FLOPS = 2 * E * B * H * (H + 2 * P)


def tile_ensembledynamicsmodel_pa_e_kernel(
    tc,
    h3,
    state,
    noise,
    W4_words,
    W4_scales,
    b4,
    W5_words,
    W5_scales,
    b5,
    max_logvar,
    min_logvar,
    out_0,
    out_1,
):
    nc = tc.nc
    with ExitStack() as ctx:
        ctx.enter_context(tc.manual_schedule())
        keep = ctx.enter_context(tc.tile_pool(name="keep", bufs=1))
        work = ctx.enter_context(tc.tile_pool(name="work", bufs=2))
        psum = ctx.enter_context(tc.psum_pool(name="psum", bufs=1))

        ident_f32 = keep.tile([P, P], F32)
        make_identity(nc, ident_f32[:])
        ident_bf16 = keep.tile([P, P], BF16)
        make_identity(nc, ident_bf16[:])

        groups = (E + GROUP - 1) // GROUP
        w4_scales_raw = keep.tile([P, groups, H], U8, align_bytes=64)
        w4_scales = keep.tile([P, groups, PACK, P], U8, align_bytes=64)
        w5_scales = keep.tile([P, groups, 2 * P], U8, align_bytes=64)
        limit_rows = keep.tile([P, P], BF16)
        nc.vector.memset(limit_rows[:], 0.0)
        warm = keep.tile([P, 1], F32)
        nc.vector.memset(warm[:], 0.0)
        zeros = keep.tile([P, N], BF16)
        nc.vector.memset(zeros[:], 0.0)
        b4_rows = keep.tile([P, H], BF16)
        nc.vector.memset(b4_rows[:], 0.0)
        b5_rows = keep.tile([P, P], BF16)
        nc.vector.memset(b5_rows[:], 0.0)
        nc.vector.memset(w4_scales_raw[:].rearrange("p g n -> p (g n)").bitcast(I32), 0)
        nc.vector.memset(w5_scales[:].rearrange("p g n -> p (g n)").bitcast(I32), 0)

        h3_sb = {}
        w4_loaded = {}
        w4_words = {}
        w5_words = {}
        noise_sb = {}

        def load_h3(e, half, pieces=1):
            rows = keep.tile([P, QUAD * H], BF16, name="h3_%d_%d" % (e, half))
            by_partition = h3[e].rearrange("(p i) k -> p (i k)", i=TILES)
            width = QUAD * H // pieces
            for piece in range(pieces):
                first = half * QUAD * H + piece * width
                nc.sync.dma_start(
                    out=rows[:, piece * width : (piece + 1) * width], in_=by_partition[:, first : first + width]
                )
            h3_sb[e, half] = rows

        def load_words(words_in, e, columns, label):
            words = keep.tile([P, columns], U32, name="%s_%d" % (label, e), align_bytes=64)
            nc.sync.dma_start(
                out=words[:].bitcast(I32),
                in_=words_in[e].rearrange("p n t -> p (n t)").bitcast(I32),
            )
            return words

        def load_scales(plane, scales_in, group):
            members = min(GROUP, E - group * GROUP)
            for quadrant in range(P // 32):
                first = quadrant * LIVE_ROWS
                nc.sync.dma_start(
                    out=plane[32 * quadrant : 32 * quadrant + members * LIVE_ROWS, group, :].bitcast(I32),
                    in_=scales_in[
                        group * GROUP : group * GROUP + members, first : first + LIVE_ROWS, :
                    ].bitcast(I32),
                )

        def load_noise(e):
            rows = keep.tile([P, TILES, P], BF16, name="noise_%d" % e)
            nc.sync.dma_start(
                out=rows[:].rearrange("p i c -> p (i c)"),
                in_=noise[e].rearrange("(p i) c -> p (i c)", i=TILES),
            )
            noise_sb[e] = rows

        nc.scalar.activation(out=warm[:], in_=warm[:], func=ACT.Exp)
        nc.sync.dma_start(out=limit_rows[0:1, :], in_=max_logvar)
        nc.sync.dma_start(out=limit_rows[1:2, :], in_=min_logvar)
        load_h3(0, 0, PAIRS)
        w4_loaded[0] = load_words(W4_words, 0, H, "w4_loaded")
        load_scales(w4_scales_raw, W4_scales, 0)
        load_h3(0, 1)
        nc.sync.dma_start(out=b4_rows[0:E, :], in_=b4)
        nc.sync.dma_start(out=b5_rows[0 : 2 * E, :], in_=b5.rearrange("e (h c) -> h e c", h=2))
        for e in range(1, E + 1):
            if e < E:
                load_h3(e, 0)
                w4_loaded[e] = load_words(W4_words, e, H, "w4_loaded")
                if e % GROUP == 0:
                    load_scales(w4_scales_raw, W4_scales, e // GROUP)
                load_h3(e, 1)
            if (e - 1) % GROUP == 0:
                load_scales(w5_scales, W5_scales, (e - 1) // GROUP)
            w5_words[e - 1] = load_words(W5_words, e - 1, 2 * P, "w5")
        for e in range(E):
            load_noise(e)
        state_sb = keep.tile([P, TILES, S], BF16)
        nc.sync.dma_start(
            out=state_sb[:].rearrange("p i s -> p (i s)"),
            in_=state.rearrange("(p i) s -> p (i s)", i=TILES),
        )

        h4_codes = {}
        h4_scales = {}
        clamped = {}
        noise_t = {}
        for e in range(E):
            h4_codes[e] = keep.tile([P, B], U32, name="h4_codes_%d" % e, align_bytes=64)
            h4_scales[e] = keep.tile([P, B], U8, name="h4_scales_%d" % e, align_bytes=64)
            clamped[e] = keep.tile([P, B], F32, name="clamped_%d" % e)
            if e not in DIRECT:
                noise_t[e] = keep.tile([P, B], BF16, name="noise_t_%d" % e)
        rewards_sb = keep.tile([P, E, TILES, 1], F32)

        b4_cols = keep.tile([P, PACK, E], F32)
        b5_cols = keep.tile([P, 2 * E], F32)
        limit_cols = keep.tile([P, 2], F32)
        exps = keep.tile([P, 2], F32)
        half_emax = keep.tile([P, 1], F32)
        var_mid = keep.tile([P, 1], F32)
        tanh_bias = keep.tile([P, E], F32)

        def columns_of_limits():
            limit_ps = psum.tile([P, P], BF16, tag="tl")
            nc.tensor.transpose(limit_ps[:], limit_rows[:], ident_bf16[:])
            nc.vector.tensor_copy(out=limit_cols[:], in_=limit_ps[:, 0:2])
            nc.scalar.activation(out=exps[:], in_=limit_cols[:], func=ACT.Exp)

        def columns_of_biases():
            b4_ps = psum.tile([P, PACK, P], BF16, tag="a3", name="b4_ps")
            for t in range(PACK):
                nc.tensor.transpose(b4_ps[:, t, :], b4_rows[:, t::PACK], ident_bf16[:])
            b5_ps = psum.tile([P, P], BF16, tag="tl")
            nc.tensor.transpose(b5_ps[:], b5_rows[:], ident_bf16[:])
            nc.vector.tensor_copy(out=b4_cols[:], in_=b4_ps[:, :, 0:E])
            nc.vector.tensor_copy(out=b5_cols[:], in_=b5_ps[:, 0 : 2 * E])
            nc.vector.tensor_scalar(
                out=tanh_bias[:],
                in0=b5_cols[:, E : 2 * E],
                scalar1=limit_cols[:, 0:1],
                scalar2=0.5,
                op0=ALU.subtract,
                op1=ALU.mult,
            )
            nc.vector.tensor_scalar_mul(out=half_emax[:], in0=exps[:, 0:1], scalar1=0.5)
            nc.vector.tensor_add(out=var_mid[:], in0=exps[:, 1:2], in1=half_emax[:])

        def reorder_w4_scales(group):
            nc.vector.tensor_copy(
                out=w4_scales[:, group], in_=w4_scales_raw[:, group, :].rearrange("p (m t) -> p t m", t=PACK)
            )

        def reorder_w4(e):
            words = keep.tile([P, PACK, P], U32, name="w4_%d" % e, align_bytes=64)
            nc.vector.tensor_copy(
                out=words[:].bitcast(I32),
                in_=w4_loaded[e][:].bitcast(I32).rearrange("p (m t) -> p t m", t=PACK),
            )
            w4_words[e] = words

        live = {}

        def member_of(s):
            return s // HALVES

        def columns_of(s):
            half = s % HALVES
            return slice(half * N, (half + 1) * N)

        def transpose_h3(s, pair):
            words = h3_sb[divmod(s, HALVES)][:].bitcast(F32)
            xt = psum.tile([P, PAIR, 2, P], F32, tag="x%d" % ((s * PAIRS + pair) % X_BANKS), name="xt")
            for i in range(PAIR):
                first = (pair * PAIR + i) * (H // 2)
                for u in range(2):
                    nc.tensor.transpose(xt[:, i, u, :], words[:, first + u : first + H // 2 : 2], ident_f32[:])
            live["xt", s, pair] = xt

        def copy_h3(copy, s, pair):
            if pair == 0:
                live["h3_grouped", s] = work.tile([P, N * PACK], BF16, tag="h3_grouped", name="h3_grouped", align_bytes=64)
            width = PAIR * P * PACK
            copy(
                out=live["h3_grouped", s][:, pair * width : (pair + 1) * width]
                .bitcast(F32)
                .rearrange("p (i b u) -> p i b u", i=PAIR, u=2),
                in_=live["xt", s, pair][:].rearrange("p i u b -> p i b u"),
            )

        def quantise_h3(s):
            codes = work.tile([P, N], U32, tag="h3_codes", align_bytes=64)
            scales = work.tile([P, N], U8, tag="h3_scales", align_bytes=64)
            nc.vector.quantize_mx(out=codes[:].bitcast(FP8X4), scales=scales[:], in_=live["h3_grouped", s][:])
            live["h3_mx", s] = (codes, scales)

        def layer4(s, t):
            e = member_of(s)
            group, slot = divmod(e, GROUP)
            codes, scales = live["h3_mx", s]
            acc = psum.tile([P, N], F32, tag="a%d" % t, name="acc")
            nc.tensor.matmul_mx(
                out=acc[:],
                lhsT=w4_words[e][:, t, :].bitcast(FP8X4),
                lhsT_scale=w4_scales[slot * LIVE_ROWS : P, group, t, :],
                rhs=codes[:].bitcast(FP8X4),
                rhs_scale=scales[:],
                start=True,
                stop=True,
            )
            live["acc", s, t] = acc

        def swish(s):
            e = member_of(s)
            h4 = work.tile([P, PACK, N], BF16, tag="h4")
            for t in range(PACK):
                if t == PACK - 1:
                    if member_of(s - 2) < LATE:
                        stage(clamp_tanh, s - 2)
                nc.scalar.activation(
                    out=h4[:, t, :], in_=live["acc", s, t][:], func=ACT.Silu, bias=b4_cols[:, t, e : e + 1]
                )
            live["h4", s] = h4

        def interleave_h4(s):
            grouped = work.tile([P, N, PACK], BF16, tag="h4_grouped", align_bytes=64)
            nc.vector.tensor_copy(
                out=grouped[:].rearrange("p (c i) t -> p c t i", i=PACK),
                in_=live["h4", s][:].rearrange("p t (c i) -> p c t i", i=PACK),
            )
            live["h4_grouped", s] = grouped

        def quantise_h4(s):
            e, cols = member_of(s), columns_of(s)
            nc.vector.quantize_mx(
                out=h4_codes[e][:, cols].bitcast(FP8X4),
                scales=h4_scales[e][:, cols],
                in_=live["h4_grouped", s][:].rearrange("p b t -> p (b t)"),
            )

        def w5_pass(out, e, first, cols):
            group, slot = divmod(e, GROUP)
            nc.tensor.matmul_mx(
                out=out,
                lhsT=w5_words[e][:, first : first + P].bitcast(FP8X4),
                lhsT_scale=w5_scales[slot * LIVE_ROWS : P, group, first : first + P],
                rhs=h4_codes[e][:, cols].bitcast(FP8X4),
                rhs_scale=h4_scales[e][:, cols],
                start=True,
                stop=True,
            )

        def logvar(s, bank="tl"):
            lv = psum.tile([P, N], F32, tag=bank, name="lv")
            w5_pass(lv[:], member_of(s), P, columns_of(s))
            live["lv", s] = lv

        def clamp_tanh(s):
            e, cols = member_of(s), columns_of(s)
            nc.scalar.activation(
                out=clamped[e][:, cols],
                in_=live["lv", s][:],
                func=ACT.Tanh,
                bias=tanh_bias[:, e : e + 1],
                scale=0.5,
            )

        def transpose_noise(e):
            noise_ps = psum.tile([P, TILES, P], BF16, tag=("x2", "tl")[e in (2, 4, 6)], name="noise_ps")
            for i in range(TILES):
                nc.tensor.matmul(
                    out=noise_ps[:, i, :], lhsT=noise_sb[e][:, i, :], rhs=ident_bf16[:], start=True, stop=True
                )
            live["noise_ps", e] = noise_ps

        def copy_noise(copy, e):
            copy(out=noise_t[e][:], in_=live["noise_ps", e][:].rearrange("p i b -> p (i b)"))

        def stage(function, s, *args):
            if 0 <= s < STEPS:
                function(s, *args)

        def first_part_round(r):
            if r > 0:
                stage(layer4, r, 0)
                stage(layer4, r, 1)
            stage(transpose_h3, r + 2, 0)
            if r > 0:
                stage(layer4, r, 2)
                stage(layer4, r, 3)
            if member_of(r - 2) < LATE:
                stage(logvar, r - 2)
            stage(transpose_h3, r + 2, 1)
            stage(quantise_h3, r + 1)
            stage(swish, r)
            stage(interleave_h4, r - 1)
            if 0 <= r + 2 < STEPS:
                copy_h3(nc.vector.tensor_copy, r + 2, 0)
            if 0 <= r + 2 < STEPS:
                copy_h3(nc.scalar.copy, r + 2, 1)
            stage(quantise_h4, r - 1)
            if r + 2 == STEPS:
                transpose_noise(1)
                copy_noise(nc.vector.tensor_copy, 1)
            e, half = divmod(r + 2, HALVES)
            if half == 0 and 0 < e < E:
                reorder_w4(e)
                if e % GROUP == 0:
                    reorder_w4_scales(e // GROUP)

        def warm_up():
            for t in range(PACK - 1):
                scratch = psum.tile([P, N], F32, tag="a%d" % t, name="scratch")
                nc.tensor.matmul(out=scratch[:], lhsT=zeros[:, 0:P], rhs=zeros[:], start=True, stop=True)

        warm_up()
        columns_of_limits()
        for pair in range(PAIRS):
            transpose_h3(0, pair)
        copy_h3(nc.vector.tensor_copy, 0, 0)
        copy_h3(nc.scalar.copy, 0, 1)
        nc.scalar.activation(out=warm[:], in_=exps[:, 0:1], func=ACT.Silu)
        reorder_w4(0)
        reorder_w4_scales(0)
        quantise_h3(0)
        columns_of_biases()
        layer4(0, 0)
        layer4(0, 1)
        transpose_h3(1, 0)
        copy_h3(nc.scalar.copy, 1, 0)
        layer4(0, 2)
        layer4(0, 3)
        transpose_h3(1, 1)
        copy_h3(nc.vector.tensor_copy, 1, 1)
        for r in range(STEPS):
            first_part_round(r)

        def half_columns(half):
            return slice(half * N, (half + 1) * N)

        def stds(e):
            for half in range(HALVES):
                cols = half_columns(half)
                nc.scalar.activation(
                    out=clamped[e][:, cols], in_=clamped[e][:, cols], func=ACT.Sqrt, bias=var_mid[:], scale=half_emax[:]
                )

        def spread_noise(e):
            for half in range(HALVES):
                cols = half_columns(half)
                if e in DIRECT:
                    nc.vector.tensor_tensor(
                        out=clamped[e][:, cols],
                        in0=live["noise_ps", e][:, half * QUAD : (half + 1) * QUAD, :].rearrange("p i b -> p (i b)"),
                        in1=clamped[e][:, cols],
                        op=ALU.mult,
                    )
                else:
                    nc.gpsimd.tensor_tensor(
                        out=clamped[e][:, cols], in0=clamped[e][:, cols], in1=noise_t[e][:, cols], op=ALU.mult
                    )

        def mean(e):
            for half in range(HALVES):
                mean_ps = psum.tile([P, N], F32, tag="a%d" % half, name="mean_ps")
                w5_pass(mean_ps[:], e, 0, half_columns(half))
                live["mean", e, half] = mean_ps

        def sample(e):
            for half in range(HALVES):
                samples = work.tile([P, N], F32, tag="samples", bufs=2 * HALVES)
                nc.vector.scalar_tensor_tensor(
                    out=samples[:],
                    in0=live["mean", e, half][:],
                    scalar=b5_cols[:, e : e + 1],
                    in1=clamped[e][:, half_columns(half)],
                    op0=ALU.add,
                    op1=ALU.add,
                )
                live["samples", e, half] = samples

        def transpose_back(e):
            for half in range(HALVES):
                samples = live["samples", e, half]
                back = psum.tile([P, QUAD, P], F32, tag="x%d" % half, name="back")
                for j in range(QUAD):
                    nc.tensor.transpose(back[:, j, :], samples[:, j * P : (j + 1) * P], ident_f32[:])
                live["back", e, half] = back

        def store_rewards(first, last):
            nc.sync.dma_start(
                out=out_1[first:last].rearrange("e (p i) o -> p e (i o)", i=TILES),
                in_=rewards_sb[:, first:last].rearrange("p e i o -> p e (i o)"),
            )

        def finish(e):
            next_states = work.tile([P, TILES, S], F32, tag="next_states", bufs=3)
            for half in range(HALVES):
                tiles = slice(half * QUAD, (half + 1) * QUAD)
                back = live["back", e, half]
                nc.vector.tensor_tensor(
                    out=next_states[:, tiles, :], in0=back[:, :, 0:S], in1=state_sb[:, tiles, :], op=ALU.add
                )
                nc.vector.tensor_copy(out=rewards_sb[:, e, tiles, :], in_=back[:, :, S : S + 1])
            nc.sync.dma_start(
                out=out_0[e].rearrange("(p i) s -> p (i s)", i=TILES),
                in_=next_states[:].rearrange("p i s -> p (i s)"),
            )
            if e == E - 2:
                store_rewards(0, E - 1)

        def member_stage(function, e):
            if 0 <= e < E:
                function(e)

        transpose_noise(0)
        transpose_noise(2)
        interleave_h4(STEPS - 1)
        quantise_h4(STEPS - 1)
        for e in range(3):
            stds(e)
        def late_logvars(e):
            for half in range(HALVES):
                logvar(e * HALVES + half, ("a2", "a3")[half])

        def late_tanhs(e):
            for half in range(HALVES):
                clamp_tanh(e * HALVES + half)

        mean(0)
        late_logvars(LATE)
        for r in range(-1, E):
            if r >= 0:
                member_stage(mean, r + 1)
            member_stage(spread_noise, r + 1)
            member_stage(transpose_back, r)
            member_stage(transpose_noise, r + 4)
            if r + 4 < LATE:
                stds(r + 4)
            if r + 4 < E and r + 4 not in DIRECT:
                copy_noise(nc.scalar.copy, r + 4)
            if r + 4 == LATE:
                late_tanhs(LATE)
            if r + 4 == LATE + 1:
                late_logvars(LATE + 1)
                late_tanhs(LATE + 1)
                stds(LATE)
                stds(LATE + 1)
            member_stage(sample, r + 1)
            if r == -1:
                copy_noise(nc.vector.tensor_copy, 2)
            member_stage(finish, r)

        store_rewards(E - 1, E)
